import numpy as np
import ml_dtypes


def mxq(x, axis, fmt="e4m3"):
    dtype, down = {"e4m3": (ml_dtypes.float8_e4m3fn, 7), "e5m2": (ml_dtypes.float8_e5m2, 14)}[fmt]
    v = np.moveaxis(np.asarray(x, np.float32).astype(ml_dtypes.bfloat16).astype(np.float64), axis, -1)
    blocks = v.reshape(v.shape[:-1] + (-1, 32))
    amax = np.abs(blocks).max(-1, keepdims=True)
    byte = np.maximum(np.where(amax > 0, np.frexp(amax)[1] - 1 + 127, 0) - down, 1)
    scale = np.exp2(byte - 127.0)
    codes = (blocks / scale).astype(np.float32).astype(dtype).astype(np.float64)
    return np.moveaxis((codes * scale).reshape(v.shape), -1, axis)


WIDE = False


def mx_kscale(k):
    if not WIDE:
        return np.ones(k)
    levels = np.array([10, -10, 5, -5, 0])
    a = np.random.permutation(np.resize(levels, k // 512 * 4)).reshape(k // 512, 4)
    idx = np.arange(k)
    return np.exp2(a[idx // 512, idx % 128 // 32])


BF16 = ml_dtypes.bfloat16


def bf(x):
    return np.asarray(x, np.float32).astype(BF16)


def f64(x):
    return np.asarray(x).astype(np.float64)


B, N, F = 2, 512, 1024
OUT = F


def setup_inputs():
    s = mx_kscale(N)
    adj = np.random.uniform(0.0, 1.0, (N, N))
    adj = adj / adj.sum(axis=1, keepdims=True) * np.sqrt(N)
    return {"prott5_emd": bf(np.random.standard_normal((B, N, F)) / s[None, :, None]),
            "adj": bf(adj * s[None, :]),
            "h0": bf(np.random.standard_normal((B, N, F))),
            "weight": bf(np.random.uniform(-1.0, 1.0, (F, OUT)) * 1.7 / np.sqrt(F)),
            "lamda": 0.5, "alpha": 0.1, "l": 1}


def reference(prott5_emd, adj, h0, weight, lamda, alpha, l):
    theta = min(1.0, np.log(lamda / l + 1.0))
    hi = mxq(f64(adj), 1, "e4m3") @ mxq(f64(prott5_emd), 1, "e4m3")
    support = (1.0 - alpha) * hi + alpha * f64(h0)
    return theta * (mxq(support, 2, "e4m3") @ mxq(f64(weight), 0, "e4m3")) + (1.0 - theta) * support

@@ -1,0 +1,277 @@
+import math
+from contextlib import ExitStack
+
+import concourse.mybir as mybir
+from concourse.masks import make_identity
+
+FLOPS = 2 * 2 * 512 * 512 * 1024 + 2 * 2 * 512 * 1024 * 1024
+
+F32 = mybir.dt.float32
+BF16 = mybir.dt.bfloat16
+U32 = mybir.dt.uint32
+U8 = mybir.dt.uint8
+FP8X4 = mybir.dt.float8_e4m3fn_x4
+MULT = mybir.AluOpType.mult
+ADD = mybir.AluOpType.add
+COPY = mybir.ActivationFunctionType.Copy
+
+P = 128
+HALF = 512
+PIN = False
+
+
+def tile_graphconvolution_kernel(tc, prott5_emd, adj, h0, weight, lamda, alpha, l, out):
+    nc = tc.nc
+    theta = min(1.0, math.log(lamda / l + 1.0))
+    assert alpha > 0.0
+    hi_gain = (1.0 - alpha) / alpha
+    res_gain = (1.0 - theta) * alpha
+    units = [(0, 0), (0, 1), (1, 0), (1, 1)]
+
+    with ExitStack() as ctx:
+        keep = ctx.enter_context(tc.tile_pool(name="keep", bufs=1))
+        accp = ctx.enter_context(tc.psum_pool(name="accp", bufs=4))
+        tpp = ctx.enter_context(tc.psum_pool(name="tpp", bufs=4))
+        if PIN:
+            ctx.enter_context(tc.manual_schedule())
+
+        ident = keep.tile([P, P], F32, name="ident")
+        make_identity(nc, ident[:])
+
+        adj_sb = keep.tile([P, 4 * 512], BF16, name="adj_sb")
+        agr = keep.tile([P, 2048], BF16, name="agr", align_bytes=64)
+        a_codes = keep.tile([P, 512], U32, name="a_codes", align_bytes=64)
+        a_plane = keep.tile([P, 512], U8, name="a_plane", align_bytes=64)
+        xraw, xgr, x_codes, x_plane = {}, {}, {}, {}
+        h0_sb, t_sb, r_sb = {}, {}, {}
+        sgr, s_codes, s_plane = {}, {}, {}
+        wraw, wgr, w_codes, w_plane = {}, {}, {}, {}
+        for u in units:
+            tagn = "%d%d" % u
+            xraw[u] = keep.tile([P, 4, HALF], BF16, name="xraw" + tagn)
+            xgr[u] = keep.tile([P, HALF, 4], BF16, name="xgr" + tagn, align_bytes=64)
+            x_codes[u] = keep.tile([P, HALF], U32, name="xc" + tagn, align_bytes=64)
+            x_plane[u] = keep.tile([P, HALF], U8, name="xs" + tagn, align_bytes=64)
+            h0_sb[u] = keep.tile([P, 4, HALF], BF16, name="h0" + tagn)
+            t_sb[u] = keep.tile([P, 4, HALF], F32, name="t" + tagn)
+            r_sb[u] = keep.tile([P, 4, HALF], F32, name="r" + tagn)
+            sgr[u] = keep.tile([P, 4, P, 4], BF16, name="sgr" + tagn, align_bytes=64)
+            s_codes[u] = keep.tile([P, HALF], U32, name="sc" + tagn, align_bytes=64)
+            s_plane[u] = keep.tile([P, HALF], U8, name="ss" + tagn, align_bytes=64)
+            wraw[u] = keep.tile([P, 4, HALF], BF16, name="wraw" + tagn)
+            wgr[u] = keep.tile([P, HALF, 4], BF16, name="wgr" + tagn, align_bytes=64)
+            w_codes[u] = keep.tile([P, HALF], U32, name="wc" + tagn, align_bytes=64)
+            w_plane[u] = keep.tile([P, HALF], U8, name="ws" + tagn, align_bytes=64)
+
+        nc.sync.dma_start(
+            out=adj_sb[:].rearrange("p (i m) -> p i m", i=4),
+            in_=adj.rearrange("(i p) m -> p i m", p=P),
+        )
+        for (b, h) in units:
+            cols = slice(HALF * h, HALF * h + HALF)
+            nc.sync.dma_start(
+                out=xraw[(b, h)][:],
+                in_=prott5_emd[b].rearrange("(p j) f -> p j f", j=4)[:, :, cols],
+            )
+            nc.sync.dma_start(
+                out=h0_sb[(b, h)][:],
+                in_=h0[b].rearrange("(i p) f -> p i f", p=P)[:, :, cols],
+            )
+        for (c, h) in [(0, 0), (1, 0), (0, 1), (1, 1)]:
+            nc.sync.dma_start(
+                out=wraw[(c, h)][:],
+                in_=weight[HALF * c : HALF * c + HALF, HALF * h : HALF * h + HALF].rearrange(
+                    "(j p) o -> p j o", p=P
+                ),
+            )
+
+        def regroup(eng, dst, src):
+            if eng == "v":
+                nc.vector.tensor_copy(
+                    out=dst[:].rearrange("p (c i) t -> p c t i", i=4),
+                    in_=src[:].rearrange("p t (c i) -> p c t i", i=4),
+                )
+            elif eng == "s":
+                nc.scalar.copy(
+                    out=dst[:].rearrange("p (c i) t -> p c t i", i=4),
+                    in_=src[:].rearrange("p t (c i) -> p c t i", i=4),
+                )
+            else:
+                nc.gpsimd.tensor_scalar(
+                    out=dst[:],
+                    in0=src[:].rearrange("p t w -> p w t"),
+                    scalar1=1.0,
+                    scalar2=0.0,
+                    op0=MULT,
+                    op1=ADD,
+                )
+
+        def quant(codes, plane, grouped2d):
+            nc.vector.quantize_mx(out=codes[:].bitcast(FP8X4), scales=plane[:], in_=grouped2d)
+
+        def quant_x(u):
+            quant(x_codes[u], x_plane[u], xgr[u][:].rearrange("p w j -> p (w j)"))
+
+        def quant_w(u):
+            quant(w_codes[u], w_plane[u], wgr[u][:].rearrange("p w j -> p (w j)"))
+
+        def quant_s(u):
+            quant(s_codes[u], s_plane[u], sgr[u][:].rearrange("p i n j -> p (i n j)"))
+
+        acc = {}
+
+        def stage1(u, blocks):
+            for i in blocks:
+                a = accp.tile([P, HALF], F32, name="acc1_%d%d%d" % (u[0], u[1], i), tag="acc")
+                acc[(1, u, i)] = a
+                nc.tensor.matmul_mx(
+                    out=a[:],
+                    lhsT=a_codes[:, P * i : P * i + P].bitcast(FP8X4),
+                    lhsT_scale=a_plane[:, P * i : P * i + P],
+                    rhs=x_codes[u][:].bitcast(FP8X4),
+                    rhs_scale=x_plane[u][:],
+                    start=True,
+                    stop=True,
+                )
+
+        def combine(u, blocks):
+            for i in blocks:
+                nc.vector.scalar_tensor_tensor(
+                    out=t_sb[u][:, i, :],
+                    in0=acc[(1, u, i)][:],
+                    scalar=hi_gain,
+                    in1=h0_sb[u][:, i, :],
+                    op0=MULT,
+                    op1=ADD,
+                )
+
+        def turn(u):
+            tps = []
+            for i in range(4):
+                tp = tpp.tile([P, 4, P], F32, name="tp_%d%d%d" % (u[0], u[1], i), tag="tp")
+                tps.append(tp)
+                for j in range(4):
+                    nc.tensor.transpose(tp[:, j, :], t_sb[u][:, i, P * j : P * j + P], ident[:])
+            for i in range(4):
+                nc.scalar.activation(
+                    out=sgr[u][:, i, :, :],
+                    in_=tps[i][:].rearrange("p j n -> p n j"),
+                    func=COPY,
+                    scale=alpha,
+                )
+
+        def rescale(eng, u):
+            dst = r_sb[u][:].rearrange("p i f -> p (i f)")
+            src = t_sb[u][:].rearrange("p i f -> p (i f)")
+            if eng == "g":
+                nc.gpsimd.tensor_scalar(out=dst, in0=src, scalar1=res_gain, scalar2=0.0, op0=MULT, op1=ADD)
+            else:
+                nc.scalar.activation(out=dst, in_=src, func=COPY, scale=res_gain)
+
+        def stage2(u, blocks):
+            b, h = u
+            for i in blocks:
+                a = accp.tile([P, HALF], F32, name="acc2_%d%d%d" % (b, h, i), tag="acc")
+                acc[(2, u, i)] = a
+                for c in range(2):
+                    nc.tensor.matmul_mx(
+                        out=a[:],
+                        lhsT=s_codes[(b, c)][:, P * i : P * i + P].bitcast(FP8X4),
+                        lhsT_scale=s_plane[(b, c)][:, P * i : P * i + P],
+                        rhs=w_codes[(c, h)][:].bitcast(FP8X4),
+                        rhs_scale=w_plane[(c, h)][:],
+                        start=(c == 0),
+                        stop=(c == 1),
+                    )
+
+        def finish(u, blocks):
+            b, h = u
+            for i in blocks:
+                nc.vector.scalar_tensor_tensor(
+                    out=t_sb[u][:, i, :],
+                    in0=acc[(2, u, i)][:],
+                    scalar=theta,
+                    in1=r_sb[u][:, i, :],
+                    op0=MULT,
+                    op1=ADD,
+                )
+                nc.sync.dma_start(
+                    out=out[b, P * i : P * i + P, HALF * h : HALF * h + HALF],
+                    in_=t_sb[u][:, i, :],
+                )
+
+        adj_words = adj_sb[:].bitcast(F32).rearrange("p (i w u) -> p i w u", i=4, u=2)
+        agr_words = agr[:].bitcast(F32).rearrange("p (n u) -> p n u", u=2)
+        pa = []
+        for hn in range(2):
+            t2 = tpp.tile([P, 2, 256], F32, name="pa%d" % hn, tag="tp")
+            pa.append(t2)
+            for k in range(2):
+                for u in range(2):
+                    nc.tensor.transpose(t2[:, u, P * k : P * k + P], adj_words[:, 2 * hn + k, :, u], ident[:])
+        for hn in range(2):
+            nc.scalar.copy(
+                out=agr_words[:, 256 * hn : 256 * hn + 256, :],
+                in_=pa[hn][:].rearrange("p u n -> p n u"),
+            )
+
+        U0, U1, U2, U3 = units
+        regroup("v", xgr[U0], xraw[U0])
+        regroup("s", xgr[U1], xraw[U1])
+        quant(a_codes, a_plane, agr[:])
+        quant_x(U0)
+        stage1(U0, [0, 1, 2, 3])
+        combine(U0, [0, 1])
+        quant_x(U1)
+        stage1(U1, [0, 1])
+        combine(U0, [2, 3])
+        stage1(U1, [2, 3])
+        regroup("s", xgr[U2], xraw[U2])
+        regroup("g", xgr[U3], xraw[U3])
+        turn(U0)
+        combine(U1, [0, 1])
+        quant_x(U2)
+        stage1(U2, [0, 1])
+        combine(U1, [2, 3])
+        stage1(U2, [2, 3])
+        regroup("s", wgr[(0, 0)], wraw[(0, 0)])
+        regroup("g", wgr[(1, 0)], wraw[(1, 0)])
+        turn(U1)
+        quant_s(U0)
+        combine(U2, [0, 1])
+        quant_x(U3)
+        stage1(U3, [0, 1])
+        combine(U2, [2, 3])
+        stage1(U3, [2, 3])
+        regroup("s", wgr[(0, 1)], wraw[(0, 1)])
+        regroup("g", wgr[(1, 1)], wraw[(1, 1)])
+        turn(U2)
+        quant_s(U1)
+        combine(U3, [0, 1])
+        quant_w((0, 0))
+        quant_w((1, 0))
+        stage2(U0, [0, 1])
+        combine(U3, [2, 3])
+        stage2(U0, [2, 3])
+        rescale("g", U0)
+        turn(U3)
+        quant_w((0, 1))
+        quant_w((1, 1))
+        finish(U0, [0, 1])
+        stage2(U1, [0, 1])
+        quant_s(U2)
+        finish(U0, [2, 3])
+        stage2(U1, [2, 3])
+        rescale("g", U1)
+        rescale("s", U2)
+        quant_s(U3)
+        finish(U1, [0, 1])
+        stage2(U2, [0, 1])
+        finish(U1, [2, 3])
+        stage2(U2, [2, 3])
+        rescale("s", U3)
+        finish(U2, [0, 1])
+        stage2(U3, [0, 1])
+        finish(U2, [2, 3])
+        stage2(U3, [2, 3])
+        finish(U3, [0, 1, 2, 3])

@@ -227,7 +227,7 @@ def tile_graphconvolution_kernel(tc, prott5_emd, adj, h0, weight, lamda, alpha, 
         combine(U0, [2, 3])
         stage1(U1, [2, 3])
         regroup("s", xgr[U2], xraw[U2])
-        regroup("g", xgr[U3], xraw[U3])
+        regroup("v", xgr[U3], xraw[U3])
         turn(U0)
         combine(U1, [0, 1])
         quant_x(U2)
@@ -235,7 +235,7 @@ def tile_graphconvolution_kernel(tc, prott5_emd, adj, h0, weight, lamda, alpha, 
         combine(U1, [2, 3])
         stage1(U2, [2, 3])
         regroup("s", wgr[(0, 0)], wraw[(0, 0)])
-        regroup("g", wgr[(1, 0)], wraw[(1, 0)])
+        regroup("v", wgr[(1, 0)], wraw[(1, 0)])
         turn(U1)
         quant_s(U0)
         combine(U2, [0, 1])
@@ -244,7 +244,7 @@ def tile_graphconvolution_kernel(tc, prott5_emd, adj, h0, weight, lamda, alpha, 
         combine(U2, [2, 3])
         stage1(U3, [2, 3])
         regroup("s", wgr[(0, 1)], wraw[(0, 1)])
-        regroup("g", wgr[(1, 1)], wraw[(1, 1)])
+        regroup("v", wgr[(1, 1)], wraw[(1, 1)])
         turn(U2)
         quant_s(U1)
         combine(U3, [0, 1])
@@ -253,7 +253,7 @@ def tile_graphconvolution_kernel(tc, prott5_emd, adj, h0, weight, lamda, alpha, 
         stage2(U0, [0, 1])
         combine(U3, [2, 3])
         stage2(U0, [2, 3])
-        rescale("g", U0)
+        rescale("s", U0)
         turn(U3)
         quant_w((0, 1))
         quant_w((1, 1))
@@ -262,7 +262,7 @@ def tile_graphconvolution_kernel(tc, prott5_emd, adj, h0, weight, lamda, alpha, 
         quant_s(U2)
         finish(U0, [2, 3])
         stage2(U1, [2, 3])
-        rescale("g", U1)
+        rescale("s", U1)
         rescale("s", U2)
         quant_s(U3)
         finish(U1, [0, 1])

@@ -17,7 +17,7 @@ COPY = mybir.ActivationFunctionType.Copy
 
 P = 128
 HALF = 512
-PIN = False
+PIN = True
 
 
 def tile_graphconvolution_kernel(tc, prott5_emd, adj, h0, weight, lamda, alpha, l, out):
@@ -227,7 +227,7 @@ def tile_graphconvolution_kernel(tc, prott5_emd, adj, h0, weight, lamda, alpha, 
         combine(U0, [2, 3])
         stage1(U1, [2, 3])
         regroup("s", xgr[U2], xraw[U2])
-        regroup("v", xgr[U3], xraw[U3])
+        regroup("g", xgr[U3], xraw[U3])
         turn(U0)
         combine(U1, [0, 1])
         quant_x(U2)
@@ -235,7 +235,7 @@ def tile_graphconvolution_kernel(tc, prott5_emd, adj, h0, weight, lamda, alpha, 
         combine(U1, [2, 3])
         stage1(U2, [2, 3])
         regroup("s", wgr[(0, 0)], wraw[(0, 0)])
-        regroup("v", wgr[(1, 0)], wraw[(1, 0)])
+        regroup("g", wgr[(1, 0)], wraw[(1, 0)])
         turn(U1)
         quant_s(U0)
         combine(U2, [0, 1])
@@ -244,7 +244,7 @@ def tile_graphconvolution_kernel(tc, prott5_emd, adj, h0, weight, lamda, alpha, 
         combine(U2, [2, 3])
         stage1(U3, [2, 3])
         regroup("s", wgr[(0, 1)], wraw[(0, 1)])
-        regroup("v", wgr[(1, 1)], wraw[(1, 1)])
+        regroup("g", wgr[(1, 1)], wraw[(1, 1)])
         turn(U2)
         quant_s(U1)
         combine(U3, [0, 1])
@@ -253,7 +253,7 @@ def tile_graphconvolution_kernel(tc, prott5_emd, adj, h0, weight, lamda, alpha, 
         stage2(U0, [0, 1])
         combine(U3, [2, 3])
         stage2(U0, [2, 3])
-        rescale("s", U0)
+        rescale("g", U0)
         turn(U3)
         quant_w((0, 1))
         quant_w((1, 1))
@@ -262,7 +262,7 @@ def tile_graphconvolution_kernel(tc, prott5_emd, adj, h0, weight, lamda, alpha, 
         quant_s(U2)
         finish(U0, [2, 3])
         stage2(U1, [2, 3])
-        rescale("s", U1)
+        rescale("g", U1)
         rescale("s", U2)
         quant_s(U3)
         finish(U1, [0, 1])

@@ -17,23 +17,67 @@ COPY = mybir.ActivationFunctionType.Copy
 
 P = 128
 HALF = 512
-PIN = True
+
+SCHEDULE = [
+    ("ld", "adj"), ("ld", "X00"), ("ld", "h00"), ("ta", 0),
+    ("ta", 1), ("ld", "X01"), ("eva", 0, "s"), ("rx", (0, 0), "v"),
+    ("eva", 1, "s"), ("ld", "X10"), ("qa",), ("ps", (0, 0), 0, "g"),
+    ("qx", (0, 0)), ("ld", "h01"), ("ps", (0, 0), 1, "g"), ("rx", (0, 1), "s"),
+    ("s1", (0, 0), 0), ("s1", (0, 0), 1), ("ld", "h10"), ("s1", (0, 0), 2),
+    ("p1", (0, 0), 0), ("s1", (0, 0), 3), ("rx", (1, 0), "g"), ("p1", (0, 0), 1),
+    ("t", (0, 0), 0), ("ld", "X11"), ("p1", (0, 0), 2), ("t", (0, 0), 1),
+    ("evt", (0, 0), 0), ("qx", (0, 1)), ("t", (0, 0), 2), ("evt", (0, 0), 1),
+    ("ld", "W00"), ("p1", (0, 0), 3), ("evt", (0, 0), 2), ("s1", (0, 1), 0),
+    ("ps", (0, 1), 0, "g"), ("ps", (0, 1), 1, "v"), ("s1", (0, 1), 1), ("ps", (1, 0), 0, "s"),
+    ("ld", "W10"), ("s1", (0, 1), 2), ("qx", (1, 0)), ("s1", (0, 1), 3),
+    ("t", (0, 0), 3), ("rx", (1, 1), "g"), ("p1", (0, 1), 2), ("ps", (1, 0), 1, "s"),
+    ("ld", "h11"), ("p1", (0, 1), 0), ("t", (0, 1), 2), ("evt", (0, 0), 3),
+    ("p1", (0, 1), 1), ("t", (0, 1), 0), ("ld", "W01"), ("s1", (1, 0), 0),
+    ("evt", (0, 1), 2), ("p1", (0, 1), 3), ("s1", (1, 0), 1), ("s1", (1, 0), 2),
+    ("evt", (0, 1), 0), ("qs", (0, 0)), ("rw", (0, 0), "g"), ("t", (0, 1), 1),
+    ("ld", "W11"), ("rw", (1, 0), "s"), ("t", (0, 1), 3), ("qx", (1, 1)),
+    ("s1", (1, 0), 3), ("p1", (1, 0), 0), ("p1", (1, 0), 1), ("s1", (1, 1), 0),
+    ("t", (1, 0), 0), ("p1", (1, 0), 2), ("evt", (0, 1), 1), ("t", (1, 0), 1),
+    ("ps", (1, 1), 0, "g"), ("s1", (1, 1), 1), ("qw", (0, 0)), ("evt", (0, 1), 3),
+    ("s1", (1, 1), 2), ("t", (1, 0), 2), ("p1", (1, 0), 3), ("evt", (1, 0), 0),
+    ("ps", (1, 1), 1, "g"), ("qs", (0, 1)), ("evt", (1, 0), 1), ("t", (1, 0), 3),
+    ("s1", (1, 1), 3), ("qw", (1, 0)), ("evt", (1, 0), 2), ("rw", (1, 1), "g"),
+    ("p1", (1, 1), 0), ("evt", (1, 0), 3), ("rw", (0, 1), "s"), ("p1", (1, 1), 1),
+    ("s2", (0, 0), 0), ("qs", (1, 0)), ("t", (1, 1), 0), ("t", (1, 1), 1),
+    ("p1", (1, 1), 2), ("s2", (0, 0), 1), ("p1", (1, 1), 3), ("s2", (0, 0), 2),
+    ("fe", (0, 0), 0), ("qw", (0, 1)), ("s2", (0, 0), 3), ("fe", (0, 0), 1),
+    ("fg", (0, 0), 0), ("qw", (1, 1)), ("t", (1, 1), 2), ("evt", (1, 1), 0),
+    ("t", (1, 1), 3), ("fv", (0, 0), 2), ("evt", (1, 1), 1), ("s2", (0, 1), 0),
+    ("fg", (0, 0), 1), ("st", (0, 0), 0), ("fv", (0, 0), 3), ("evt", (1, 1), 2),
+    ("s2", (0, 1), 1), ("st", (0, 0), 2), ("evt", (1, 1), 3), ("fv", (0, 1), 0),
+    ("s2", (0, 1), 2), ("st", (0, 0), 3), ("fe", (0, 1), 1), ("qs", (1, 1)),
+    ("s2", (0, 1), 3), ("st", (0, 0), 1), ("fv", (0, 1), 2), ("fg", (0, 1), 1),
+    ("st", (0, 1), 0), ("fe", (0, 1), 3), ("s2", (1, 0), 0), ("st", (0, 1), 2),
+    ("s2", (1, 0), 1), ("fg", (0, 1), 3), ("fv", (1, 0), 0), ("st", (0, 1), 1),
+    ("s2", (1, 0), 2), ("fe", (1, 0), 1), ("s2", (1, 0), 3), ("st", (1, 0), 0),
+    ("fv", (1, 0), 2), ("fg", (1, 0), 1), ("s2", (1, 1), 0), ("st", (0, 1), 3),
+    ("fv", (1, 0), 3), ("s2", (1, 1), 1), ("st", (1, 0), 2), ("fe", (1, 1), 0),
+    ("s2", (1, 1), 2), ("st", (1, 0), 3), ("fv", (1, 1), 1), ("fg", (1, 1), 0),
+    ("s2", (1, 1), 3), ("st", (1, 0), 1), ("fv", (1, 1), 2), ("st", (1, 1), 1),
+    ("fv", (1, 1), 3), ("st", (1, 1), 0), ("st", (1, 1), 2), ("st", (1, 1), 3),
+]
 
 
 def tile_graphconvolution_kernel(tc, prott5_emd, adj, h0, weight, lamda, alpha, l, out):
     nc = tc.nc
     theta = min(1.0, math.log(lamda / l + 1.0))
-    assert alpha > 0.0
-    hi_gain = (1.0 - alpha) / alpha
-    res_gain = (1.0 - theta) * alpha
+    assert 0.0 < alpha and theta < 1.0
+    hi_gain = (1.0 - alpha) * (1.0 - theta)
+    h0_gain = alpha * (1.0 - theta)
+    back_gain = 1.0 / (1.0 - theta)
     units = [(0, 0), (0, 1), (1, 0), (1, 1)]
 
     with ExitStack() as ctx:
         keep = ctx.enter_context(tc.tile_pool(name="keep", bufs=1))
+        stage = ctx.enter_context(tc.tile_pool(name="stage", bufs=3))
         accp = ctx.enter_context(tc.psum_pool(name="accp", bufs=4))
         tpp = ctx.enter_context(tc.psum_pool(name="tpp", bufs=4))
-        if PIN:
-            ctx.enter_context(tc.manual_schedule())
+        ctx.enter_context(tc.manual_schedule())
 
         ident = keep.tile([P, P], F32, name="ident")
         make_identity(nc, ident[:])
@@ -43,7 +87,7 @@ def tile_graphconvolution_kernel(tc, prott5_emd, adj, h0, weight, lamda, alpha, 
         a_codes = keep.tile([P, 512], U32, name="a_codes", align_bytes=64)
         a_plane = keep.tile([P, 512], U8, name="a_plane", align_bytes=64)
         xraw, xgr, x_codes, x_plane = {}, {}, {}, {}
-        h0_sb, t_sb, r_sb = {}, {}, {}
+        h0_sb, r_sb = {}, {}
         sgr, s_codes, s_plane = {}, {}, {}
         wraw, wgr, w_codes, w_plane = {}, {}, {}, {}
         for u in units:
@@ -53,7 +97,6 @@ def tile_graphconvolution_kernel(tc, prott5_emd, adj, h0, weight, lamda, alpha, 
             x_codes[u] = keep.tile([P, HALF], U32, name="xc" + tagn, align_bytes=64)
             x_plane[u] = keep.tile([P, HALF], U8, name="xs" + tagn, align_bytes=64)
             h0_sb[u] = keep.tile([P, 4, HALF], BF16, name="h0" + tagn)
-            t_sb[u] = keep.tile([P, 4, HALF], F32, name="t" + tagn)
             r_sb[u] = keep.tile([P, 4, HALF], F32, name="r" + tagn)
             sgr[u] = keep.tile([P, 4, P, 4], BF16, name="sgr" + tagn, align_bytes=64)
             s_codes[u] = keep.tile([P, HALF], U32, name="sc" + tagn, align_bytes=64)
@@ -63,27 +106,45 @@ def tile_graphconvolution_kernel(tc, prott5_emd, adj, h0, weight, lamda, alpha, 
             w_codes[u] = keep.tile([P, HALF], U32, name="wc" + tagn, align_bytes=64)
             w_plane[u] = keep.tile([P, HALF], U8, name="ws" + tagn, align_bytes=64)
 
-        nc.sync.dma_start(
-            out=adj_sb[:].rearrange("p (i m) -> p i m", i=4),
-            in_=adj.rearrange("(i p) m -> p i m", p=P),
-        )
-        for (b, h) in units:
+        adj_words = adj_sb[:].bitcast(F32).rearrange("p (i w u) -> p i w u", i=4, u=2)
+        agr_words = agr[:].bitcast(F32).rearrange("p (n u) -> p n u", u=2)
+        live = {}
+
+        def ld(name):
+            if name == "adj":
+                nc.sync.dma_start(out=adj_sb[:], in_=adj.rearrange("(p i) m -> p (i m)", i=4))
+                return
+            a = int(name[1])
+            h = int(name[2])
             cols = slice(HALF * h, HALF * h + HALF)
-            nc.sync.dma_start(
-                out=xraw[(b, h)][:],
-                in_=prott5_emd[b].rearrange("(p j) f -> p j f", j=4)[:, :, cols],
-            )
-            nc.sync.dma_start(
-                out=h0_sb[(b, h)][:],
-                in_=h0[b].rearrange("(i p) f -> p i f", p=P)[:, :, cols],
-            )
-        for (c, h) in [(0, 0), (1, 0), (0, 1), (1, 1)]:
-            nc.sync.dma_start(
-                out=wraw[(c, h)][:],
-                in_=weight[HALF * c : HALF * c + HALF, HALF * h : HALF * h + HALF].rearrange(
-                    "(j p) o -> p j o", p=P
-                ),
-            )
+            if name[0] == "X":
+                nc.sync.dma_start(
+                    out=xraw[(a, h)][:], in_=prott5_emd[a].rearrange("(p j) f -> p j f", j=4)[:, :, cols]
+                )
+            elif name[0] == "h":
+                nc.sync.dma_start(
+                    out=h0_sb[(a, h)][:], in_=h0[a].rearrange("(p i) f -> p i f", i=4)[:, :, cols]
+                )
+            else:
+                nc.sync.dma_start(
+                    out=wraw[(a, h)][:],
+                    in_=weight[HALF * a : HALF * a + HALF, cols].rearrange("(j p) o -> p j o", p=P),
+                )
+
+        def ta(hn):
+            t2 = tpp.tile([P, 2, 256], F32, name="pa%d" % hn, tag="tp")
+            live[("pa", hn)] = t2
+            for k in range(2):
+                for w in range(2):
+                    nc.tensor.transpose(t2[:, w, P * k : P * k + P], adj_words[:, 2 * hn + k, :, w], ident[:])
+
+        def eva(hn, eng):
+            dst = agr_words[:, 256 * hn : 256 * hn + 256, :]
+            src = live[("pa", hn)][:].rearrange("p u n -> p n u")
+            if eng == "s":
+                nc.scalar.copy(out=dst, in_=src)
+            else:
+                nc.vector.tensor_copy(out=dst, in_=src)
 
         def regroup(eng, dst, src):
             if eng == "v":
@@ -98,180 +159,110 @@ def tile_graphconvolution_kernel(tc, prott5_emd, adj, h0, weight, lamda, alpha, 
                 )
             else:
                 nc.gpsimd.tensor_scalar(
-                    out=dst[:],
-                    in0=src[:].rearrange("p t w -> p w t"),
-                    scalar1=1.0,
-                    scalar2=0.0,
-                    op0=MULT,
-                    op1=ADD,
+                    out=dst[:], in0=src[:].rearrange("p t w -> p w t"), scalar1=1.0, scalar2=0.0, op0=MULT, op1=ADD
                 )
 
         def quant(codes, plane, grouped2d):
             nc.vector.quantize_mx(out=codes[:].bitcast(FP8X4), scales=plane[:], in_=grouped2d)
 
-        def quant_x(u):
+        def qa():
+            quant(a_codes, a_plane, agr[:])
+
+        def rx(u, eng):
+            regroup(eng, xgr[u], xraw[u])
+
+        def rw(u, eng):
+            regroup(eng, wgr[u], wraw[u])
+
+        def qx(u):
             quant(x_codes[u], x_plane[u], xgr[u][:].rearrange("p w j -> p (w j)"))
 
-        def quant_w(u):
+        def qw(u):
             quant(w_codes[u], w_plane[u], wgr[u][:].rearrange("p w j -> p (w j)"))
 
-        def quant_s(u):
+        def qs(u):
             quant(s_codes[u], s_plane[u], sgr[u][:].rearrange("p i n j -> p (i n j)"))
 
-        acc = {}
-
-        def stage1(u, blocks):
-            for i in blocks:
-                a = accp.tile([P, HALF], F32, name="acc1_%d%d%d" % (u[0], u[1], i), tag="acc")
-                acc[(1, u, i)] = a
-                nc.tensor.matmul_mx(
-                    out=a[:],
-                    lhsT=a_codes[:, P * i : P * i + P].bitcast(FP8X4),
-                    lhsT_scale=a_plane[:, P * i : P * i + P],
-                    rhs=x_codes[u][:].bitcast(FP8X4),
-                    rhs_scale=x_plane[u][:],
-                    start=True,
-                    stop=True,
-                )
-
-        def combine(u, blocks):
-            for i in blocks:
-                nc.vector.scalar_tensor_tensor(
-                    out=t_sb[u][:, i, :],
-                    in0=acc[(1, u, i)][:],
-                    scalar=hi_gain,
-                    in1=h0_sb[u][:, i, :],
-                    op0=MULT,
-                    op1=ADD,
-                )
-
-        def turn(u):
-            tps = []
-            for i in range(4):
-                tp = tpp.tile([P, 4, P], F32, name="tp_%d%d%d" % (u[0], u[1], i), tag="tp")
-                tps.append(tp)
-                for j in range(4):
-                    nc.tensor.transpose(tp[:, j, :], t_sb[u][:, i, P * j : P * j + P], ident[:])
-            for i in range(4):
-                nc.scalar.activation(
-                    out=sgr[u][:, i, :, :],
-                    in_=tps[i][:].rearrange("p j n -> p n j"),
-                    func=COPY,
-                    scale=alpha,
-                )
-
-        def rescale(eng, u):
-            dst = r_sb[u][:].rearrange("p i f -> p (i f)")
-            src = t_sb[u][:].rearrange("p i f -> p (i f)")
+        def ps(u, hp, eng):
+            dst = r_sb[u][:, 2 * hp : 2 * hp + 2, :]
+            src = h0_sb[u][:, 2 * hp : 2 * hp + 2, :]
             if eng == "g":
-                nc.gpsimd.tensor_scalar(out=dst, in0=src, scalar1=res_gain, scalar2=0.0, op0=MULT, op1=ADD)
+                nc.gpsimd.tensor_scalar(out=dst, in0=src, scalar1=h0_gain, scalar2=0.0, op0=MULT, op1=ADD)
+            elif eng == "v":
+                nc.vector.tensor_scalar(out=dst, in0=src, scalar1=h0_gain, scalar2=0.0, op0=MULT, op1=ADD)
             else:
-                nc.scalar.activation(out=dst, in_=src, func=COPY, scale=res_gain)
+                nc.scalar.activation(out=dst, in_=src, func=COPY, scale=h0_gain)
 
-        def stage2(u, blocks):
-            b, h = u
-            for i in blocks:
-                a = accp.tile([P, HALF], F32, name="acc2_%d%d%d" % (b, h, i), tag="acc")
-                acc[(2, u, i)] = a
-                for c in range(2):
-                    nc.tensor.matmul_mx(
-                        out=a[:],
-                        lhsT=s_codes[(b, c)][:, P * i : P * i + P].bitcast(FP8X4),
-                        lhsT_scale=s_plane[(b, c)][:, P * i : P * i + P],
-                        rhs=w_codes[(c, h)][:].bitcast(FP8X4),
-                        rhs_scale=w_plane[(c, h)][:],
-                        start=(c == 0),
-                        stop=(c == 1),
-                    )
-
-        def finish(u, blocks):
-            b, h = u
-            for i in blocks:
-                nc.vector.scalar_tensor_tensor(
-                    out=t_sb[u][:, i, :],
-                    in0=acc[(2, u, i)][:],
-                    scalar=theta,
-                    in1=r_sb[u][:, i, :],
-                    op0=MULT,
-                    op1=ADD,
-                )
-                nc.sync.dma_start(
-                    out=out[b, P * i : P * i + P, HALF * h : HALF * h + HALF],
-                    in_=t_sb[u][:, i, :],
-                )
-
-        adj_words = adj_sb[:].bitcast(F32).rearrange("p (i w u) -> p i w u", i=4, u=2)
-        agr_words = agr[:].bitcast(F32).rearrange("p (n u) -> p n u", u=2)
-        pa = []
-        for hn in range(2):
-            t2 = tpp.tile([P, 2, 256], F32, name="pa%d" % hn, tag="tp")
-            pa.append(t2)
-            for k in range(2):
-                for u in range(2):
-                    nc.tensor.transpose(t2[:, u, P * k : P * k + P], adj_words[:, 2 * hn + k, :, u], ident[:])
-        for hn in range(2):
-            nc.scalar.copy(
-                out=agr_words[:, 256 * hn : 256 * hn + 256, :],
-                in_=pa[hn][:].rearrange("p u n -> p n u"),
+        def s1(u, i):
+            a = accp.tile([P, HALF], F32, name="acc1_%d%d%d" % (u[0], u[1], i), tag="acc")
+            live[(1, u, i)] = a
+            nc.tensor.matmul_mx(
+                out=a[:],
+                lhsT=a_codes[:, P * i : P * i + P].bitcast(FP8X4),
+                lhsT_scale=a_plane[:, P * i : P * i + P],
+                rhs=x_codes[u][:].bitcast(FP8X4),
+                rhs_scale=x_plane[u][:],
+                start=True,
+                stop=True,
             )
 
-        U0, U1, U2, U3 = units
-        regroup("v", xgr[U0], xraw[U0])
-        regroup("s", xgr[U1], xraw[U1])
-        quant(a_codes, a_plane, agr[:])
-        quant_x(U0)
-        stage1(U0, [0, 1, 2, 3])
-        combine(U0, [0, 1])
-        quant_x(U1)
-        stage1(U1, [0, 1])
-        combine(U0, [2, 3])
-        stage1(U1, [2, 3])
-        regroup("s", xgr[U2], xraw[U2])
-        regroup("g", xgr[U3], xraw[U3])
-        turn(U0)
-        combine(U1, [0, 1])
-        quant_x(U2)
-        stage1(U2, [0, 1])
-        combine(U1, [2, 3])
-        stage1(U2, [2, 3])
-        regroup("s", wgr[(0, 0)], wraw[(0, 0)])
-        regroup("g", wgr[(1, 0)], wraw[(1, 0)])
-        turn(U1)
-        quant_s(U0)
-        combine(U2, [0, 1])
-        quant_x(U3)
-        stage1(U3, [0, 1])
-        combine(U2, [2, 3])
-        stage1(U3, [2, 3])
-        regroup("s", wgr[(0, 1)], wraw[(0, 1)])
-        regroup("g", wgr[(1, 1)], wraw[(1, 1)])
-        turn(U2)
-        quant_s(U1)
-        combine(U3, [0, 1])
-        quant_w((0, 0))
-        quant_w((1, 0))
-        stage2(U0, [0, 1])
-        combine(U3, [2, 3])
-        stage2(U0, [2, 3])
-        rescale("g", U0)
-        turn(U3)
-        quant_w((0, 1))
-        quant_w((1, 1))
-        finish(U0, [0, 1])
-        stage2(U1, [0, 1])
-        quant_s(U2)
-        finish(U0, [2, 3])
-        stage2(U1, [2, 3])
-        rescale("g", U1)
-        rescale("s", U2)
-        quant_s(U3)
-        finish(U1, [0, 1])
-        stage2(U2, [0, 1])
-        finish(U1, [2, 3])
-        stage2(U2, [2, 3])
-        rescale("s", U3)
-        finish(U2, [0, 1])
-        stage2(U3, [0, 1])
-        finish(U2, [2, 3])
-        stage2(U3, [2, 3])
-        finish(U3, [0, 1, 2, 3])
+        def p1(u, i):
+            nc.vector.scalar_tensor_tensor(
+                out=r_sb[u][:, i, :], in0=live[(1, u, i)][:], scalar=hi_gain, in1=r_sb[u][:, i, :], op0=MULT, op1=ADD
+            )
+
+        def t(u, i):
+            tp = tpp.tile([P, 4, P], F32, name="tp_%d%d%d" % (u[0], u[1], i), tag="tp")
+            live[("tp", u, i)] = tp
+            for j in range(4):
+                nc.tensor.transpose(tp[:, j, :], r_sb[u][:, i, P * j : P * j + P], ident[:])
+
+        def evt(u, i):
+            nc.scalar.activation(
+                out=sgr[u][:, i, :, :],
+                in_=live[("tp", u, i)][:].rearrange("p j n -> p n j"),
+                func=COPY,
+                scale=back_gain,
+            )
+
+        def s2(u, i):
+            b, h = u
+            a = accp.tile([P, HALF], F32, name="acc2_%d%d%d" % (b, h, i), tag="acc")
+            live[(2, u, i)] = a
+            for c in range(2):
+                nc.tensor.matmul_mx(
+                    out=a[:],
+                    lhsT=s_codes[(b, c)][:, P * i : P * i + P].bitcast(FP8X4),
+                    lhsT_scale=s_plane[(b, c)][:, P * i : P * i + P],
+                    rhs=w_codes[(c, h)][:].bitcast(FP8X4),
+                    rhs_scale=w_plane[(c, h)][:],
+                    start=(c == 0),
+                    stop=(c == 1),
+                )
+
+        def fv(u, i):
+            nc.vector.scalar_tensor_tensor(
+                out=r_sb[u][:, i, :], in0=live[(2, u, i)][:], scalar=theta, in1=r_sb[u][:, i, :], op0=MULT, op1=ADD
+            )
+
+        def fe(u, i):
+            ut = stage.tile([P, HALF], F32, name="u_%d%d%d" % (u[0], u[1], i), tag="u")
+            live[("u", u, i)] = ut
+            nc.scalar.activation(out=ut[:], in_=live[(2, u, i)][:], func=COPY, scale=theta)
+
+        def fg(u, i):
+            nc.gpsimd.tensor_tensor(out=r_sb[u][:, i, :], in0=live[("u", u, i)][:], in1=r_sb[u][:, i, :], op=ADD)
+
+        def st(u, i):
+            b, h = u
+            nc.sync.dma_start(
+                out=out[b].rearrange("(p i) o -> p i o", i=4)[:, i, HALF * h : HALF * h + HALF],
+                in_=r_sb[u][:, i, :],
+            )
+
+        table = {
+            "ld": ld, "ta": ta, "eva": eva, "qa": qa, "rx": rx, "rw": rw, "qx": qx, "qw": qw, "qs": qs, "ps": ps,
+            "s1": s1, "p1": p1, "t": t, "evt": evt, "s2": s2, "fv": fv, "fe": fe, "fg": fg, "st": st,
+        }
+        for step in SCHEDULE:
+            table[step[0]](*step[1:])

@@ -19,47 +19,45 @@ P = 128
 HALF = 512
 
 SCHEDULE = [
-    ("ld", "adj"), ("ld", "X00"), ("ld", "h00"), ("ta", 0),
-    ("ta", 1), ("ld", "X01"), ("eva", 0, "s"), ("rx", (0, 0), "v"),
-    ("eva", 1, "s"), ("ld", "X10"), ("qa",), ("ps", (0, 0), 0, "g"),
-    ("qx", (0, 0)), ("ld", "h01"), ("ps", (0, 0), 1, "g"), ("rx", (0, 1), "s"),
-    ("s1", (0, 0), 0), ("s1", (0, 0), 1), ("ld", "h10"), ("s1", (0, 0), 2),
-    ("p1", (0, 0), 0), ("s1", (0, 0), 3), ("rx", (1, 0), "g"), ("p1", (0, 0), 1),
-    ("t", (0, 0), 0), ("ld", "X11"), ("p1", (0, 0), 2), ("t", (0, 0), 1),
-    ("evt", (0, 0), 0), ("qx", (0, 1)), ("t", (0, 0), 2), ("evt", (0, 0), 1),
-    ("ld", "W00"), ("p1", (0, 0), 3), ("evt", (0, 0), 2), ("s1", (0, 1), 0),
-    ("ps", (0, 1), 0, "g"), ("ps", (0, 1), 1, "v"), ("s1", (0, 1), 1), ("ps", (1, 0), 0, "s"),
-    ("ld", "W10"), ("s1", (0, 1), 2), ("qx", (1, 0)), ("s1", (0, 1), 3),
-    ("t", (0, 0), 3), ("rx", (1, 1), "g"), ("p1", (0, 1), 2), ("ps", (1, 0), 1, "s"),
-    ("ld", "h11"), ("p1", (0, 1), 0), ("t", (0, 1), 2), ("evt", (0, 0), 3),
-    ("p1", (0, 1), 1), ("t", (0, 1), 0), ("ld", "W01"), ("s1", (1, 0), 0),
-    ("evt", (0, 1), 2), ("p1", (0, 1), 3), ("s1", (1, 0), 1), ("s1", (1, 0), 2),
-    ("evt", (0, 1), 0), ("qs", (0, 0)), ("rw", (0, 0), "g"), ("t", (0, 1), 1),
-    ("ld", "W11"), ("rw", (1, 0), "s"), ("t", (0, 1), 3), ("qx", (1, 1)),
-    ("s1", (1, 0), 3), ("p1", (1, 0), 0), ("p1", (1, 0), 1), ("s1", (1, 1), 0),
-    ("t", (1, 0), 0), ("p1", (1, 0), 2), ("evt", (0, 1), 1), ("t", (1, 0), 1),
-    ("ps", (1, 1), 0, "g"), ("s1", (1, 1), 1), ("qw", (0, 0)), ("evt", (0, 1), 3),
-    ("s1", (1, 1), 2), ("t", (1, 0), 2), ("p1", (1, 0), 3), ("evt", (1, 0), 0),
-    ("ps", (1, 1), 1, "g"), ("qs", (0, 1)), ("evt", (1, 0), 1), ("t", (1, 0), 3),
-    ("s1", (1, 1), 3), ("qw", (1, 0)), ("evt", (1, 0), 2), ("rw", (1, 1), "g"),
-    ("p1", (1, 1), 0), ("evt", (1, 0), 3), ("rw", (0, 1), "s"), ("p1", (1, 1), 1),
-    ("s2", (0, 0), 0), ("qs", (1, 0)), ("t", (1, 1), 0), ("t", (1, 1), 1),
-    ("p1", (1, 1), 2), ("s2", (0, 0), 1), ("p1", (1, 1), 3), ("s2", (0, 0), 2),
-    ("fe", (0, 0), 0), ("qw", (0, 1)), ("s2", (0, 0), 3), ("fe", (0, 0), 1),
-    ("fg", (0, 0), 0), ("qw", (1, 1)), ("t", (1, 1), 2), ("evt", (1, 1), 0),
-    ("t", (1, 1), 3), ("fv", (0, 0), 2), ("evt", (1, 1), 1), ("s2", (0, 1), 0),
-    ("fg", (0, 0), 1), ("st", (0, 0), 0), ("fv", (0, 0), 3), ("evt", (1, 1), 2),
-    ("s2", (0, 1), 1), ("st", (0, 0), 2), ("evt", (1, 1), 3), ("fv", (0, 1), 0),
-    ("s2", (0, 1), 2), ("st", (0, 0), 3), ("fe", (0, 1), 1), ("qs", (1, 1)),
-    ("s2", (0, 1), 3), ("st", (0, 0), 1), ("fv", (0, 1), 2), ("fg", (0, 1), 1),
-    ("st", (0, 1), 0), ("fe", (0, 1), 3), ("s2", (1, 0), 0), ("st", (0, 1), 2),
-    ("s2", (1, 0), 1), ("fg", (0, 1), 3), ("fv", (1, 0), 0), ("st", (0, 1), 1),
-    ("s2", (1, 0), 2), ("fe", (1, 0), 1), ("s2", (1, 0), 3), ("st", (1, 0), 0),
-    ("fv", (1, 0), 2), ("fg", (1, 0), 1), ("s2", (1, 1), 0), ("st", (0, 1), 3),
-    ("fv", (1, 0), 3), ("s2", (1, 1), 1), ("st", (1, 0), 2), ("fe", (1, 1), 0),
-    ("s2", (1, 1), 2), ("st", (1, 0), 3), ("fv", (1, 1), 1), ("fg", (1, 1), 0),
-    ("s2", (1, 1), 3), ("st", (1, 0), 1), ("fv", (1, 1), 2), ("st", (1, 1), 1),
-    ("fv", (1, 1), 3), ("st", (1, 1), 0), ("st", (1, 1), 2), ("st", (1, 1), 3),
+    ("ld", "adj"), ("ld", "X00"), ("ld", "X01"), ("ta", 0),
+    ("ld", "X10"), ("ta", 1), ("rx", (0, 0), "v"), ("eva", 0, "s"),
+    ("ld", "h00"), ("qx", (0, 0)), ("eva", 1, "s"), ("rx", (0, 1), "s"),
+    ("ld", "h11"), ("qa",), ("s1", (0, 0), 1), ("ld", "X11"),
+    ("s1", (0, 0), 2), ("rx", (1, 0), "s"), ("p1", (0, 0), 1), ("s1", (0, 0), 0),
+    ("ld", "h01"), ("qx", (0, 1)), ("s1", (0, 0), 3), ("p1", (0, 0), 2),
+    ("ld", "W00"), ("s1", (0, 1), 3), ("p1", (0, 0), 3), ("s1", (0, 1), 1),
+    ("rx", (1, 1), "g"), ("t", (0, 0), 2), ("p1", (0, 0), 0), ("ld", "h10"),
+    ("evt", (0, 0), 2), ("qx", (1, 0)), ("t", (0, 0), 0), ("s1", (0, 1), 0),
+    ("p1", (0, 1), 1), ("evt", (0, 0), 0), ("ld", "W10"), ("s1", (1, 0), 2),
+    ("p1", (0, 1), 3), ("rw", (0, 0), "s"), ("p1", (0, 1), 0), ("s1", (1, 0), 1),
+    ("ld", "W01"), ("t", (0, 1), 3), ("qx", (1, 1)), ("s1", (0, 1), 2),
+    ("p1", (1, 0), 2), ("s1", (1, 0), 3), ("t", (0, 0), 3), ("ld", "W11"),
+    ("p1", (1, 0), 1), ("evt", (0, 1), 3), ("t", (0, 1), 0), ("s1", (1, 1), 3),
+    ("rw", (1, 0), "g"), ("qw", (0, 0)), ("evt", (0, 0), 3), ("s1", (1, 0), 0),
+    ("t", (0, 0), 1), ("p1", (1, 0), 3), ("evt", (0, 1), 0), ("t", (0, 1), 1),
+    ("p1", (0, 1), 2), ("evt", (0, 1), 1), ("p1", (1, 1), 3), ("t", (0, 1), 2),
+    ("evt", (0, 0), 1), ("t", (1, 0), 2), ("rw", (1, 1), "g"), ("p1", (1, 0), 0),
+    ("s1", (1, 1), 2), ("evt", (0, 1), 2), ("s1", (1, 1), 1), ("qw", (1, 0)),
+    ("rw", (0, 1), "s"), ("s1", (1, 1), 0), ("t", (1, 0), 1), ("qs", (0, 0)),
+    ("t", (1, 1), 3), ("qs", (0, 1)), ("p1", (1, 1), 2), ("rs", (0, 0), "g"),
+    ("s2", (0, 0), 3), ("evt", (1, 0), 2), ("p1", (1, 1), 1), ("s2", (0, 0), 0),
+    ("evt", (1, 0), 1), ("p1", (1, 1), 0), ("t", (1, 0), 3), ("evt", (1, 1), 3),
+    ("qw", (0, 1)), ("t", (1, 0), 0), ("t", (1, 1), 1), ("evt", (1, 0), 3),
+    ("qw", (1, 1)), ("rs", (0, 1), "g"), ("t", (1, 1), 0), ("evt", (1, 0), 0),
+    ("s2", (0, 0), 2), ("fv", (0, 0), 3), ("evt", (1, 1), 0), ("s2", (0, 1), 1),
+    ("fv", (0, 0), 0), ("st", (0, 0), 3), ("evt", (1, 1), 1), ("s2", (0, 1), 2),
+    ("qs", (1, 0)), ("t", (1, 1), 2), ("fv", (0, 0), 2), ("s2", (0, 0), 1),
+    ("evt", (1, 1), 2), ("fv", (0, 1), 2), ("s2", (0, 1), 3), ("rs", (1, 0), "s"),
+    ("fv", (0, 1), 1), ("st", (0, 1), 2), ("fv", (0, 0), 1), ("s2", (0, 1), 0),
+    ("st", (0, 1), 1), ("qs", (1, 1)), ("st", (0, 0), 2), ("fv", (0, 1), 3),
+    ("st", (0, 0), 0), ("rs", (1, 1), "s"), ("s2", (1, 0), 2), ("fv", (0, 1), 0),
+    ("st", (0, 0), 1), ("s2", (1, 0), 0), ("st", (0, 1), 3), ("fv", (1, 0), 2),
+    ("s2", (1, 0), 3), ("st", (0, 1), 0), ("fv", (1, 0), 0), ("s2", (1, 1), 1),
+    ("st", (1, 0), 2), ("s2", (1, 0), 1), ("fv", (1, 0), 3), ("st", (1, 0), 0),
+    ("s2", (1, 1), 3), ("fv", (1, 1), 1), ("st", (1, 0), 3), ("s2", (1, 1), 0),
+    ("fv", (1, 0), 1), ("st", (1, 1), 1), ("s2", (1, 1), 2), ("fv", (1, 1), 3),
+    ("st", (1, 0), 1), ("fv", (1, 1), 0), ("st", (1, 1), 3), ("fv", (1, 1), 2),
+    ("st", (1, 1), 0), ("st", (1, 1), 2),
 ]
 
 
@@ -67,9 +65,9 @@ def tile_graphconvolution_kernel(tc, prott5_emd, adj, h0, weight, lamda, alpha, 
     nc = tc.nc
     theta = min(1.0, math.log(lamda / l + 1.0))
     assert 0.0 < alpha and theta < 1.0
-    hi_gain = (1.0 - alpha) * (1.0 - theta)
-    h0_gain = alpha * (1.0 - theta)
-    back_gain = 1.0 / (1.0 - theta)
+    hi_gain = (1.0 - alpha) / alpha
+    res_gain = alpha * (1.0 - theta)
+    back_gain = alpha
     units = [(0, 0), (0, 1), (1, 0), (1, 1)]
 
     with ExitStack() as ctx:
@@ -87,7 +85,7 @@ def tile_graphconvolution_kernel(tc, prott5_emd, adj, h0, weight, lamda, alpha, 
         a_codes = keep.tile([P, 512], U32, name="a_codes", align_bytes=64)
         a_plane = keep.tile([P, 512], U8, name="a_plane", align_bytes=64)
         xraw, xgr, x_codes, x_plane = {}, {}, {}, {}
-        h0_sb, r_sb = {}, {}
+        h0_sb, r_sb, t_sb = {}, {}, {}
         sgr, s_codes, s_plane = {}, {}, {}
         wraw, wgr, w_codes, w_plane = {}, {}, {}, {}
         for u in units:
@@ -98,6 +96,7 @@ def tile_graphconvolution_kernel(tc, prott5_emd, adj, h0, weight, lamda, alpha, 
             x_plane[u] = keep.tile([P, HALF], U8, name="xs" + tagn, align_bytes=64)
             h0_sb[u] = keep.tile([P, 4, HALF], BF16, name="h0" + tagn)
             r_sb[u] = keep.tile([P, 4, HALF], F32, name="r" + tagn)
+            t_sb[u] = keep.tile([P, 4, HALF], F32, name="t" + tagn)
             sgr[u] = keep.tile([P, 4, P, 4], BF16, name="sgr" + tagn, align_bytes=64)
             s_codes[u] = keep.tile([P, HALF], U32, name="sc" + tagn, align_bytes=64)
             s_plane[u] = keep.tile([P, HALF], U8, name="ss" + tagn, align_bytes=64)
@@ -183,15 +182,13 @@ def tile_graphconvolution_kernel(tc, prott5_emd, adj, h0, weight, lamda, alpha, 
         def qs(u):
             quant(s_codes[u], s_plane[u], sgr[u][:].rearrange("p i n j -> p (i n j)"))
 
-        def ps(u, hp, eng):
-            dst = r_sb[u][:, 2 * hp : 2 * hp + 2, :]
-            src = h0_sb[u][:, 2 * hp : 2 * hp + 2, :]
+        def rs(u, eng):
+            dst = r_sb[u][:].rearrange("p i f -> p (i f)")
+            src = t_sb[u][:].rearrange("p i f -> p (i f)")
             if eng == "g":
-                nc.gpsimd.tensor_scalar(out=dst, in0=src, scalar1=h0_gain, scalar2=0.0, op0=MULT, op1=ADD)
-            elif eng == "v":
-                nc.vector.tensor_scalar(out=dst, in0=src, scalar1=h0_gain, scalar2=0.0, op0=MULT, op1=ADD)
+                nc.gpsimd.tensor_scalar(out=dst, in0=src, scalar1=res_gain, scalar2=0.0, op0=MULT, op1=ADD)
             else:
-                nc.scalar.activation(out=dst, in_=src, func=COPY, scale=h0_gain)
+                nc.scalar.activation(out=dst, in_=src, func=COPY, scale=res_gain)
 
         def s1(u, i):
             a = accp.tile([P, HALF], F32, name="acc1_%d%d%d" % (u[0], u[1], i), tag="acc")
@@ -208,14 +205,14 @@ def tile_graphconvolution_kernel(tc, prott5_emd, adj, h0, weight, lamda, alpha, 
 
         def p1(u, i):
             nc.vector.scalar_tensor_tensor(
-                out=r_sb[u][:, i, :], in0=live[(1, u, i)][:], scalar=hi_gain, in1=r_sb[u][:, i, :], op0=MULT, op1=ADD
+                out=t_sb[u][:, i, :], in0=live[(1, u, i)][:], scalar=hi_gain, in1=h0_sb[u][:, i, :], op0=MULT, op1=ADD
             )
 
         def t(u, i):
             tp = tpp.tile([P, 4, P], F32, name="tp_%d%d%d" % (u[0], u[1], i), tag="tp")
             live[("tp", u, i)] = tp
             for j in range(4):
-                nc.tensor.transpose(tp[:, j, :], r_sb[u][:, i, P * j : P * j + P], ident[:])
+                nc.tensor.transpose(tp[:, j, :], t_sb[u][:, i, P * j : P * j + P], ident[:])
 
         def evt(u, i):
             nc.scalar.activation(
@@ -242,7 +239,7 @@ def tile_graphconvolution_kernel(tc, prott5_emd, adj, h0, weight, lamda, alpha, 
 
         def fv(u, i):
             nc.vector.scalar_tensor_tensor(
-                out=r_sb[u][:, i, :], in0=live[(2, u, i)][:], scalar=theta, in1=r_sb[u][:, i, :], op0=MULT, op1=ADD
+                out=t_sb[u][:, i, :], in0=live[(2, u, i)][:], scalar=theta, in1=r_sb[u][:, i, :], op0=MULT, op1=ADD
             )
 
         def fe(u, i):
@@ -251,17 +248,17 @@ def tile_graphconvolution_kernel(tc, prott5_emd, adj, h0, weight, lamda, alpha, 
             nc.scalar.activation(out=ut[:], in_=live[(2, u, i)][:], func=COPY, scale=theta)
 
         def fg(u, i):
-            nc.gpsimd.tensor_tensor(out=r_sb[u][:, i, :], in0=live[("u", u, i)][:], in1=r_sb[u][:, i, :], op=ADD)
+            nc.gpsimd.tensor_tensor(out=t_sb[u][:, i, :], in0=live[("u", u, i)][:], in1=r_sb[u][:, i, :], op=ADD)
 
         def st(u, i):
             b, h = u
             nc.sync.dma_start(
                 out=out[b].rearrange("(p i) o -> p i o", i=4)[:, i, HALF * h : HALF * h + HALF],
-                in_=r_sb[u][:, i, :],
+                in_=t_sb[u][:, i, :],
             )
 
         table = {
-            "ld": ld, "ta": ta, "eva": eva, "qa": qa, "rx": rx, "rw": rw, "qx": qx, "qw": qw, "qs": qs, "ps": ps,
+            "ld": ld, "ta": ta, "eva": eva, "qa": qa, "rx": rx, "rw": rw, "qx": qx, "qw": qw, "qs": qs, "rs": rs,
             "s1": s1, "p1": p1, "t": t, "evt": evt, "s2": s2, "fv": fv, "fe": fe, "fg": fg, "st": st,
         }
         for step in SCHEDULE:

@@ -20,44 +20,46 @@ HALF = 512
 
 SCHEDULE = [
     ("ld", "adj"), ("ld", "X00"), ("ld", "X01"), ("ta", 0),
-    ("ld", "X10"), ("ta", 1), ("rx", (0, 0), "v"), ("eva", 0, "s"),
-    ("ld", "h00"), ("qx", (0, 0)), ("eva", 1, "s"), ("rx", (0, 1), "s"),
-    ("ld", "h11"), ("qa",), ("s1", (0, 0), 1), ("ld", "X11"),
-    ("s1", (0, 0), 2), ("rx", (1, 0), "s"), ("p1", (0, 0), 1), ("s1", (0, 0), 0),
-    ("ld", "h01"), ("qx", (0, 1)), ("s1", (0, 0), 3), ("p1", (0, 0), 2),
-    ("ld", "W00"), ("s1", (0, 1), 3), ("p1", (0, 0), 3), ("s1", (0, 1), 1),
-    ("rx", (1, 1), "g"), ("t", (0, 0), 2), ("p1", (0, 0), 0), ("ld", "h10"),
-    ("evt", (0, 0), 2), ("qx", (1, 0)), ("t", (0, 0), 0), ("s1", (0, 1), 0),
-    ("p1", (0, 1), 1), ("evt", (0, 0), 0), ("ld", "W10"), ("s1", (1, 0), 2),
-    ("p1", (0, 1), 3), ("rw", (0, 0), "s"), ("p1", (0, 1), 0), ("s1", (1, 0), 1),
-    ("ld", "W01"), ("t", (0, 1), 3), ("qx", (1, 1)), ("s1", (0, 1), 2),
-    ("p1", (1, 0), 2), ("s1", (1, 0), 3), ("t", (0, 0), 3), ("ld", "W11"),
-    ("p1", (1, 0), 1), ("evt", (0, 1), 3), ("t", (0, 1), 0), ("s1", (1, 1), 3),
-    ("rw", (1, 0), "g"), ("qw", (0, 0)), ("evt", (0, 0), 3), ("s1", (1, 0), 0),
-    ("t", (0, 0), 1), ("p1", (1, 0), 3), ("evt", (0, 1), 0), ("t", (0, 1), 1),
-    ("p1", (0, 1), 2), ("evt", (0, 1), 1), ("p1", (1, 1), 3), ("t", (0, 1), 2),
-    ("evt", (0, 0), 1), ("t", (1, 0), 2), ("rw", (1, 1), "g"), ("p1", (1, 0), 0),
-    ("s1", (1, 1), 2), ("evt", (0, 1), 2), ("s1", (1, 1), 1), ("qw", (1, 0)),
-    ("rw", (0, 1), "s"), ("s1", (1, 1), 0), ("t", (1, 0), 1), ("qs", (0, 0)),
-    ("t", (1, 1), 3), ("qs", (0, 1)), ("p1", (1, 1), 2), ("rs", (0, 0), "g"),
-    ("s2", (0, 0), 3), ("evt", (1, 0), 2), ("p1", (1, 1), 1), ("s2", (0, 0), 0),
-    ("evt", (1, 0), 1), ("p1", (1, 1), 0), ("t", (1, 0), 3), ("evt", (1, 1), 3),
-    ("qw", (0, 1)), ("t", (1, 0), 0), ("t", (1, 1), 1), ("evt", (1, 0), 3),
-    ("qw", (1, 1)), ("rs", (0, 1), "g"), ("t", (1, 1), 0), ("evt", (1, 0), 0),
-    ("s2", (0, 0), 2), ("fv", (0, 0), 3), ("evt", (1, 1), 0), ("s2", (0, 1), 1),
-    ("fv", (0, 0), 0), ("st", (0, 0), 3), ("evt", (1, 1), 1), ("s2", (0, 1), 2),
-    ("qs", (1, 0)), ("t", (1, 1), 2), ("fv", (0, 0), 2), ("s2", (0, 0), 1),
-    ("evt", (1, 1), 2), ("fv", (0, 1), 2), ("s2", (0, 1), 3), ("rs", (1, 0), "s"),
-    ("fv", (0, 1), 1), ("st", (0, 1), 2), ("fv", (0, 0), 1), ("s2", (0, 1), 0),
-    ("st", (0, 1), 1), ("qs", (1, 1)), ("st", (0, 0), 2), ("fv", (0, 1), 3),
-    ("st", (0, 0), 0), ("rs", (1, 1), "s"), ("s2", (1, 0), 2), ("fv", (0, 1), 0),
-    ("st", (0, 0), 1), ("s2", (1, 0), 0), ("st", (0, 1), 3), ("fv", (1, 0), 2),
-    ("s2", (1, 0), 3), ("st", (0, 1), 0), ("fv", (1, 0), 0), ("s2", (1, 1), 1),
-    ("st", (1, 0), 2), ("s2", (1, 0), 1), ("fv", (1, 0), 3), ("st", (1, 0), 0),
-    ("s2", (1, 1), 3), ("fv", (1, 1), 1), ("st", (1, 0), 3), ("s2", (1, 1), 0),
-    ("fv", (1, 0), 1), ("st", (1, 1), 1), ("s2", (1, 1), 2), ("fv", (1, 1), 3),
-    ("st", (1, 0), 1), ("fv", (1, 1), 0), ("st", (1, 1), 3), ("fv", (1, 1), 2),
-    ("st", (1, 1), 0), ("st", (1, 1), 2),
+    ("ta", 1), ("ld", "h00"), ("eva", 0, "s"), ("rx", (0, 0), "v"),
+    ("eva", 1, "s"), ("ld", "h01"), ("qa",), ("qx", (0, 0)),
+    ("ld", "X11"), ("rx", (0, 1), "v"), ("ps", (0, 0), 0, "s"), ("s1", (0, 0), 0),
+    ("s1", (0, 0), 1), ("ld", "X10"), ("s1", (0, 0), 2), ("qx", (0, 1)),
+    ("s1", (0, 0), 3), ("ps", (0, 0), 1, "s"), ("ps", (0, 1), 0, "g"), ("p1", (0, 0), 0),
+    ("ld", "h10"), ("p1", (0, 0), 1), ("s1", (0, 1), 0), ("rx", (1, 1), "s"),
+    ("t", (0, 0), 0), ("p1", (0, 0), 2), ("ps", (0, 1), 1, "g"), ("s1", (0, 1), 1),
+    ("ld", "h11"), ("t", (0, 0), 1), ("p1", (0, 0), 3), ("s1", (0, 1), 2),
+    ("t", (0, 0), 2), ("p1", (0, 1), 0), ("ld", "W10"), ("evt", (0, 0), 0),
+    ("rx", (1, 0), "g"), ("s1", (0, 1), 3), ("p1", (0, 1), 1), ("t", (0, 0), 3),
+    ("evt", (0, 0), 1), ("t", (0, 1), 0), ("ld", "W00"), ("p1", (0, 1), 2),
+    ("evt", (0, 0), 2), ("t", (0, 1), 1), ("p1", (0, 1), 3), ("ps", (1, 1), 0, "s"),
+    ("t", (0, 1), 2), ("ld", "W01"), ("qx", (1, 1)), ("ps", (1, 1), 1, "s"),
+    ("rw", (1, 0), "v"), ("s1", (1, 1), 0), ("ld", "W11"), ("s1", (1, 1), 1),
+    ("ps", (1, 0), 0, "g"), ("s1", (1, 1), 2), ("evt", (0, 0), 3), ("p1", (1, 1), 0),
+    ("s1", (1, 1), 3), ("evt", (0, 1), 0), ("t", (0, 1), 3), ("p1", (1, 1), 1),
+    ("evt", (0, 1), 1), ("t", (1, 1), 0), ("ps", (1, 0), 1, "g"), ("p1", (1, 1), 2),
+    ("evt", (0, 1), 2), ("t", (1, 1), 1), ("p1", (1, 1), 3), ("evt", (0, 1), 3),
+    ("t", (1, 1), 2), ("qs", (0, 0)), ("rw", (0, 0), "s"), ("t", (1, 1), 3),
+    ("rw", (0, 1), "g"), ("qs", (0, 1)), ("qx", (1, 0)), ("qw", (1, 0)),
+    ("s1", (1, 0), 0), ("evt", (1, 1), 0), ("qw", (0, 0)), ("s1", (1, 0), 1),
+    ("s1", (1, 0), 2), ("evt", (1, 1), 1), ("p1", (1, 0), 0), ("s1", (1, 0), 3),
+    ("evt", (1, 1), 2), ("p1", (1, 0), 1), ("s2", (0, 0), 0), ("evt", (1, 1), 3),
+    ("t", (1, 0), 0), ("p1", (1, 0), 2), ("rw", (1, 1), "s"), ("s2", (0, 0), 1),
+    ("p1", (1, 0), 3), ("s2", (0, 0), 2), ("qs", (1, 1)), ("s2", (0, 0), 3),
+    ("qw", (0, 1)), ("t", (1, 0), 1), ("evt", (1, 0), 0), ("qw", (1, 1)),
+    ("t", (1, 0), 2), ("t", (1, 0), 3), ("fe", (0, 0), 3), ("fv", (0, 0), 0),
+    ("evt", (1, 0), 1), ("fg", (0, 0), 3), ("fv", (0, 0), 1), ("st", (0, 0), 0),
+    ("s2", (0, 1), 0), ("evt", (1, 0), 2), ("fv", (0, 0), 2), ("s2", (0, 1), 1),
+    ("st", (0, 0), 1), ("evt", (1, 0), 3), ("fv", (0, 1), 0), ("s2", (0, 1), 2),
+    ("st", (0, 0), 2), ("s2", (0, 1), 3), ("qs", (1, 0)), ("st", (0, 0), 3),
+    ("fe", (0, 1), 2), ("fv", (0, 1), 1), ("st", (0, 1), 0), ("s2", (1, 0), 0),
+    ("fg", (0, 1), 2), ("fv", (0, 1), 3), ("st", (0, 1), 1), ("s2", (1, 0), 1),
+    ("fv", (1, 0), 0), ("s2", (1, 0), 2), ("st", (0, 1), 3), ("s2", (1, 0), 3),
+    ("fv", (1, 0), 1), ("st", (1, 0), 0), ("fe", (1, 0), 2), ("s2", (1, 1), 0),
+    ("st", (0, 1), 2), ("fv", (1, 0), 3), ("fg", (1, 0), 2), ("s2", (1, 1), 1),
+    ("st", (1, 0), 1), ("fv", (1, 1), 0), ("s2", (1, 1), 2), ("st", (1, 0), 3),
+    ("s2", (1, 1), 3), ("fv", (1, 1), 1), ("st", (1, 1), 0), ("fv", (1, 1), 2),
+    ("st", (1, 0), 2), ("fv", (1, 1), 3), ("st", (1, 1), 1), ("st", (1, 1), 2),
+    ("st", (1, 1), 3),
 ]
 
 
@@ -65,9 +67,9 @@ def tile_graphconvolution_kernel(tc, prott5_emd, adj, h0, weight, lamda, alpha, 
     nc = tc.nc
     theta = min(1.0, math.log(lamda / l + 1.0))
     assert 0.0 < alpha and theta < 1.0
-    hi_gain = (1.0 - alpha) / alpha
-    res_gain = alpha * (1.0 - theta)
-    back_gain = alpha
+    hi_gain = (1.0 - alpha) * (1.0 - theta)
+    h0_gain = alpha * (1.0 - theta)
+    back_gain = 1.0 / (1.0 - theta)
     units = [(0, 0), (0, 1), (1, 0), (1, 1)]
 
     with ExitStack() as ctx:
@@ -85,7 +87,7 @@ def tile_graphconvolution_kernel(tc, prott5_emd, adj, h0, weight, lamda, alpha, 
         a_codes = keep.tile([P, 512], U32, name="a_codes", align_bytes=64)
         a_plane = keep.tile([P, 512], U8, name="a_plane", align_bytes=64)
         xraw, xgr, x_codes, x_plane = {}, {}, {}, {}
-        h0_sb, r_sb, t_sb = {}, {}, {}
+        h0_sb, r_sb = {}, {}
         sgr, s_codes, s_plane = {}, {}, {}
         wraw, wgr, w_codes, w_plane = {}, {}, {}, {}
         for u in units:
@@ -96,7 +98,6 @@ def tile_graphconvolution_kernel(tc, prott5_emd, adj, h0, weight, lamda, alpha, 
             x_plane[u] = keep.tile([P, HALF], U8, name="xs" + tagn, align_bytes=64)
             h0_sb[u] = keep.tile([P, 4, HALF], BF16, name="h0" + tagn)
             r_sb[u] = keep.tile([P, 4, HALF], F32, name="r" + tagn)
-            t_sb[u] = keep.tile([P, 4, HALF], F32, name="t" + tagn)
             sgr[u] = keep.tile([P, 4, P, 4], BF16, name="sgr" + tagn, align_bytes=64)
             s_codes[u] = keep.tile([P, HALF], U32, name="sc" + tagn, align_bytes=64)
             s_plane[u] = keep.tile([P, HALF], U8, name="ss" + tagn, align_bytes=64)
@@ -182,13 +183,15 @@ def tile_graphconvolution_kernel(tc, prott5_emd, adj, h0, weight, lamda, alpha, 
         def qs(u):
             quant(s_codes[u], s_plane[u], sgr[u][:].rearrange("p i n j -> p (i n j)"))
 
-        def rs(u, eng):
-            dst = r_sb[u][:].rearrange("p i f -> p (i f)")
-            src = t_sb[u][:].rearrange("p i f -> p (i f)")
+        def ps(u, hp, eng):
+            dst = r_sb[u][:, 2 * hp : 2 * hp + 2, :]
+            src = h0_sb[u][:, 2 * hp : 2 * hp + 2, :]
             if eng == "g":
-                nc.gpsimd.tensor_scalar(out=dst, in0=src, scalar1=res_gain, scalar2=0.0, op0=MULT, op1=ADD)
+                nc.gpsimd.tensor_scalar(out=dst, in0=src, scalar1=h0_gain, scalar2=0.0, op0=MULT, op1=ADD)
+            elif eng == "v":
+                nc.vector.tensor_scalar(out=dst, in0=src, scalar1=h0_gain, scalar2=0.0, op0=MULT, op1=ADD)
             else:
-                nc.scalar.activation(out=dst, in_=src, func=COPY, scale=res_gain)
+                nc.scalar.activation(out=dst, in_=src, func=COPY, scale=h0_gain)
 
         def s1(u, i):
             a = accp.tile([P, HALF], F32, name="acc1_%d%d%d" % (u[0], u[1], i), tag="acc")
@@ -205,14 +208,14 @@ def tile_graphconvolution_kernel(tc, prott5_emd, adj, h0, weight, lamda, alpha, 
 
         def p1(u, i):
             nc.vector.scalar_tensor_tensor(
-                out=t_sb[u][:, i, :], in0=live[(1, u, i)][:], scalar=hi_gain, in1=h0_sb[u][:, i, :], op0=MULT, op1=ADD
+                out=r_sb[u][:, i, :], in0=live[(1, u, i)][:], scalar=hi_gain, in1=r_sb[u][:, i, :], op0=MULT, op1=ADD
             )
 
         def t(u, i):
             tp = tpp.tile([P, 4, P], F32, name="tp_%d%d%d" % (u[0], u[1], i), tag="tp")
             live[("tp", u, i)] = tp
             for j in range(4):
-                nc.tensor.transpose(tp[:, j, :], t_sb[u][:, i, P * j : P * j + P], ident[:])
+                nc.tensor.transpose(tp[:, j, :], r_sb[u][:, i, P * j : P * j + P], ident[:])
 
         def evt(u, i):
             nc.scalar.activation(
@@ -239,7 +242,7 @@ def tile_graphconvolution_kernel(tc, prott5_emd, adj, h0, weight, lamda, alpha, 
 
         def fv(u, i):
             nc.vector.scalar_tensor_tensor(
-                out=t_sb[u][:, i, :], in0=live[(2, u, i)][:], scalar=theta, in1=r_sb[u][:, i, :], op0=MULT, op1=ADD
+                out=r_sb[u][:, i, :], in0=live[(2, u, i)][:], scalar=theta, in1=r_sb[u][:, i, :], op0=MULT, op1=ADD
             )
 
         def fe(u, i):
@@ -248,17 +251,17 @@ def tile_graphconvolution_kernel(tc, prott5_emd, adj, h0, weight, lamda, alpha, 
             nc.scalar.activation(out=ut[:], in_=live[(2, u, i)][:], func=COPY, scale=theta)
 
         def fg(u, i):
-            nc.gpsimd.tensor_tensor(out=t_sb[u][:, i, :], in0=live[("u", u, i)][:], in1=r_sb[u][:, i, :], op=ADD)
+            nc.gpsimd.tensor_tensor(out=r_sb[u][:, i, :], in0=live[("u", u, i)][:], in1=r_sb[u][:, i, :], op=ADD)
 
         def st(u, i):
             b, h = u
             nc.sync.dma_start(
                 out=out[b].rearrange("(p i) o -> p i o", i=4)[:, i, HALF * h : HALF * h + HALF],
-                in_=t_sb[u][:, i, :],
+                in_=r_sb[u][:, i, :],
             )
 
         table = {
-            "ld": ld, "ta": ta, "eva": eva, "qa": qa, "rx": rx, "rw": rw, "qx": qx, "qw": qw, "qs": qs, "rs": rs,
+            "ld": ld, "ta": ta, "eva": eva, "qa": qa, "rx": rx, "rw": rw, "qx": qx, "qw": qw, "qs": qs, "ps": ps,
             "s1": s1, "p1": p1, "t": t, "evt": evt, "s2": s2, "fv": fv, "fe": fe, "fg": fg, "st": st,
         }
         for step in SCHEDULE:

@@ -17,50 +17,7 @@ COPY = mybir.ActivationFunctionType.Copy
 
 P = 128
 HALF = 512
-
-SCHEDULE = [
-    ("ld", "adj"), ("ld", "X00"), ("ld", "X01"), ("ta", 0),
-    ("ta", 1), ("ld", "h00"), ("eva", 0, "s"), ("rx", (0, 0), "v"),
-    ("eva", 1, "s"), ("ld", "h01"), ("qa",), ("qx", (0, 0)),
-    ("ld", "X11"), ("rx", (0, 1), "v"), ("ps", (0, 0), 0, "s"), ("s1", (0, 0), 0),
-    ("s1", (0, 0), 1), ("ld", "X10"), ("s1", (0, 0), 2), ("qx", (0, 1)),
-    ("s1", (0, 0), 3), ("ps", (0, 0), 1, "s"), ("ps", (0, 1), 0, "g"), ("p1", (0, 0), 0),
-    ("ld", "h10"), ("p1", (0, 0), 1), ("s1", (0, 1), 0), ("rx", (1, 1), "s"),
-    ("t", (0, 0), 0), ("p1", (0, 0), 2), ("ps", (0, 1), 1, "g"), ("s1", (0, 1), 1),
-    ("ld", "h11"), ("t", (0, 0), 1), ("p1", (0, 0), 3), ("s1", (0, 1), 2),
-    ("t", (0, 0), 2), ("p1", (0, 1), 0), ("ld", "W10"), ("evt", (0, 0), 0),
-    ("rx", (1, 0), "g"), ("s1", (0, 1), 3), ("p1", (0, 1), 1), ("t", (0, 0), 3),
-    ("evt", (0, 0), 1), ("t", (0, 1), 0), ("ld", "W00"), ("p1", (0, 1), 2),
-    ("evt", (0, 0), 2), ("t", (0, 1), 1), ("p1", (0, 1), 3), ("ps", (1, 1), 0, "s"),
-    ("t", (0, 1), 2), ("ld", "W01"), ("qx", (1, 1)), ("ps", (1, 1), 1, "s"),
-    ("rw", (1, 0), "v"), ("s1", (1, 1), 0), ("ld", "W11"), ("s1", (1, 1), 1),
-    ("ps", (1, 0), 0, "g"), ("s1", (1, 1), 2), ("evt", (0, 0), 3), ("p1", (1, 1), 0),
-    ("s1", (1, 1), 3), ("evt", (0, 1), 0), ("t", (0, 1), 3), ("p1", (1, 1), 1),
-    ("evt", (0, 1), 1), ("t", (1, 1), 0), ("ps", (1, 0), 1, "g"), ("p1", (1, 1), 2),
-    ("evt", (0, 1), 2), ("t", (1, 1), 1), ("p1", (1, 1), 3), ("evt", (0, 1), 3),
-    ("t", (1, 1), 2), ("qs", (0, 0)), ("rw", (0, 0), "s"), ("t", (1, 1), 3),
-    ("rw", (0, 1), "g"), ("qs", (0, 1)), ("qx", (1, 0)), ("qw", (1, 0)),
-    ("s1", (1, 0), 0), ("evt", (1, 1), 0), ("qw", (0, 0)), ("s1", (1, 0), 1),
-    ("s1", (1, 0), 2), ("evt", (1, 1), 1), ("p1", (1, 0), 0), ("s1", (1, 0), 3),
-    ("evt", (1, 1), 2), ("p1", (1, 0), 1), ("s2", (0, 0), 0), ("evt", (1, 1), 3),
-    ("t", (1, 0), 0), ("p1", (1, 0), 2), ("rw", (1, 1), "s"), ("s2", (0, 0), 1),
-    ("p1", (1, 0), 3), ("s2", (0, 0), 2), ("qs", (1, 1)), ("s2", (0, 0), 3),
-    ("qw", (0, 1)), ("t", (1, 0), 1), ("evt", (1, 0), 0), ("qw", (1, 1)),
-    ("t", (1, 0), 2), ("t", (1, 0), 3), ("fe", (0, 0), 3), ("fv", (0, 0), 0),
-    ("evt", (1, 0), 1), ("fg", (0, 0), 3), ("fv", (0, 0), 1), ("st", (0, 0), 0),
-    ("s2", (0, 1), 0), ("evt", (1, 0), 2), ("fv", (0, 0), 2), ("s2", (0, 1), 1),
-    ("st", (0, 0), 1), ("evt", (1, 0), 3), ("fv", (0, 1), 0), ("s2", (0, 1), 2),
-    ("st", (0, 0), 2), ("s2", (0, 1), 3), ("qs", (1, 0)), ("st", (0, 0), 3),
-    ("fe", (0, 1), 2), ("fv", (0, 1), 1), ("st", (0, 1), 0), ("s2", (1, 0), 0),
-    ("fg", (0, 1), 2), ("fv", (0, 1), 3), ("st", (0, 1), 1), ("s2", (1, 0), 1),
-    ("fv", (1, 0), 0), ("s2", (1, 0), 2), ("st", (0, 1), 3), ("s2", (1, 0), 3),
-    ("fv", (1, 0), 1), ("st", (1, 0), 0), ("fe", (1, 0), 2), ("s2", (1, 1), 0),
-    ("st", (0, 1), 2), ("fv", (1, 0), 3), ("fg", (1, 0), 2), ("s2", (1, 1), 1),
-    ("st", (1, 0), 1), ("fv", (1, 1), 0), ("s2", (1, 1), 2), ("st", (1, 0), 3),
-    ("s2", (1, 1), 3), ("fv", (1, 1), 1), ("st", (1, 1), 0), ("fv", (1, 1), 2),
-    ("st", (1, 0), 2), ("fv", (1, 1), 3), ("st", (1, 1), 1), ("st", (1, 1), 2),
-    ("st", (1, 1), 3),
-]
+LATE = ()
 
 
 def tile_graphconvolution_kernel(tc, prott5_emd, adj, h0, weight, lamda, alpha, l, out):
@@ -108,6 +65,7 @@ def tile_graphconvolution_kernel(tc, prott5_emd, adj, h0, weight, lamda, alpha, 
 
         adj_words = adj_sb[:].bitcast(F32).rearrange("p (i w u) -> p i w u", i=4, u=2)
         agr_words = agr[:].bitcast(F32).rearrange("p (n u) -> p n u", u=2)
+        hold_sb = keep.tile([P, 1], U32, name="hold_sb")
         live = {}
 
         def ld(name):
@@ -207,9 +165,23 @@ def tile_graphconvolution_kernel(tc, prott5_emd, adj, h0, weight, lamda, alpha, 
             )
 
         def p1(u, i):
-            nc.vector.scalar_tensor_tensor(
-                out=r_sb[u][:, i, :], in0=live[(1, u, i)][:], scalar=hi_gain, in1=r_sb[u][:, i, :], op0=MULT, op1=ADD
-            )
+            acc = live[(1, u, i)][:]
+            r = r_sb[u][:, i, :]
+            if u in LATE:
+                nc.vector.scalar_tensor_tensor(
+                    out=r, in0=h0_sb[u][:, i, :], scalar=alpha / (1.0 - alpha), in1=acc, op0=MULT, op1=ADD
+                )
+            else:
+                nc.vector.scalar_tensor_tensor(out=r, in0=acc, scalar=hi_gain, in1=r, op0=MULT, op1=ADD)
+
+        def rs(u, hp, eng):
+            r = r_sb[u][:, 2 * hp : 2 * hp + 2, :]
+            if eng == "g":
+                nc.gpsimd.tensor_scalar(out=r, in0=r, scalar1=hi_gain, scalar2=0.0, op0=MULT, op1=ADD)
+            elif eng == "v":
+                nc.vector.tensor_scalar(out=r, in0=r, scalar1=hi_gain, scalar2=0.0, op0=MULT, op1=ADD)
+            else:
+                nc.scalar.activation(out=r, in_=r, func=COPY, scale=hi_gain)
 
         def t(u, i):
             tp = tpp.tile([P, 4, P], F32, name="tp_%d%d%d" % (u[0], u[1], i), tag="tp")
@@ -222,7 +194,7 @@ def tile_graphconvolution_kernel(tc, prott5_emd, adj, h0, weight, lamda, alpha, 
                 out=sgr[u][:, i, :, :],
                 in_=live[("tp", u, i)][:].rearrange("p j n -> p n j"),
                 func=COPY,
-                scale=back_gain,
+                scale=(1.0 - alpha) if u in LATE else back_gain,
             )
 
         def s2(u, i):
@@ -253,6 +225,18 @@ def tile_graphconvolution_kernel(tc, prott5_emd, adj, h0, weight, lamda, alpha, 
         def fg(u, i):
             nc.gpsimd.tensor_tensor(out=r_sb[u][:, i, :], in0=live[("u", u, i)][:], in1=r_sb[u][:, i, :], op=ADD)
 
+        def hold(what, u, i=0):
+            if what == "p1":
+                nc.gpsimd.tensor_copy(out=hold_sb[:].bitcast(F32), in_=r_sb[u][:, i, 0:1])
+            elif what == "qw":
+                nc.gpsimd.tensor_copy(out=hold_sb[:], in_=w_codes[u][:, 0:1])
+            elif what == "qx":
+                nc.gpsimd.tensor_copy(out=hold_sb[:], in_=x_codes[u][:, 0:1])
+            elif what == "qs":
+                nc.gpsimd.tensor_copy(out=hold_sb[:], in_=s_codes[u][:, 0:1])
+            else:
+                nc.gpsimd.tensor_copy(out=hold_sb[:], in_=wgr[u][:, 0:1, 0:2].bitcast(U32))
+
         def st(u, i):
             b, h = u
             nc.sync.dma_start(
@@ -260,9 +244,167 @@ def tile_graphconvolution_kernel(tc, prott5_emd, adj, h0, weight, lamda, alpha, 
                 in_=r_sb[u][:, i, :],
             )
 
-        table = {
-            "ld": ld, "ta": ta, "eva": eva, "qa": qa, "rx": rx, "rw": rw, "qx": qx, "qw": qw, "qs": qs, "ps": ps,
-            "s1": s1, "p1": p1, "t": t, "evt": evt, "s2": s2, "fv": fv, "fe": fe, "fg": fg, "st": st,
-        }
-        for step in SCHEDULE:
-            table[step[0]](*step[1:])
+        ld("X00")
+        rx((0, 0), "v")
+        ld("adj")
+        qx((0, 0))
+        ta(0)
+        ld("X01")
+        rx((0, 1), "v")
+        eva(0, "s")
+        ta(1)
+        ld("h00")
+        eva(1, "s")
+        ld("h01")
+        qa()
+        ps((0, 0), 0, "s")
+        s1((0, 0), 0)
+        ld("X11")
+        qx((0, 1))
+        ps((0, 0), 1, "s")
+        s1((0, 0), 1)
+        hold("qx", (0, 1))
+        ld("X10")
+        p1((0, 0), 0)
+        rx((1, 1), "s")
+        s1((0, 0), 2)
+        ps((0, 1), 0, "g")
+        ld("h10")
+        p1((0, 0), 1)
+        s1((0, 0), 3)
+        ps((0, 1), 1, "g")
+        ld("h11")
+        p1((0, 0), 2)
+        s1((0, 1), 0)
+        ps((1, 0), 0, "g")
+        ld("W10")
+        p1((0, 0), 3)
+        t((0, 0), 0)
+        ps((1, 0), 1, "g")
+        ld("W00")
+        p1((0, 1), 0)
+        evt((0, 0), 0)
+        s1((0, 1), 1)
+        ld("W01")
+        p1((0, 1), 1)
+        t((0, 0), 1)
+        ld("W11")
+        evt((0, 0), 1)
+        s1((0, 1), 2)
+        p1((0, 1), 2)
+        t((0, 0), 2)
+        evt((0, 0), 2)
+        s1((0, 1), 3)
+        p1((0, 1), 3)
+        ps((1, 1), 0, "s")
+        t((0, 0), 3)
+        qx((1, 1))
+        ps((1, 1), 1, "s")
+        t((0, 1), 0)
+        rw((1, 0), "v")
+        evt((0, 0), 3)
+        t((0, 1), 1)
+        hold("rw", (1, 0))
+        evt((0, 1), 0)
+        t((0, 1), 2)
+        rx((1, 0), "g")
+        evt((0, 1), 1)
+        s1((1, 1), 0)
+        p1((1, 1), 0)
+        evt((0, 1), 2)
+        s1((1, 1), 1)
+        p1((1, 1), 1)
+        s1((1, 1), 2)
+        p1((1, 1), 2)
+        s1((1, 1), 3)
+        p1((1, 1), 3)
+        t((0, 1), 3)
+        qs((0, 0))
+        evt((0, 1), 3)
+        t((1, 1), 0)
+        qs((0, 1))
+        rw((0, 0), "s")
+        t((1, 1), 1)
+        qx((1, 0))
+        evt((1, 1), 0)
+        t((1, 1), 2)
+        qw((1, 0))
+        evt((1, 1), 1)
+        t((1, 1), 3)
+        qw((0, 0))
+        evt((1, 1), 2)
+        s1((1, 0), 0)
+        hold("qw", (0, 0))
+        p1((1, 0), 0)
+        evt((1, 1), 3)
+        s1((1, 0), 1)
+        rw((0, 1), "g")
+        p1((1, 0), 1)
+        rw((1, 1), "s")
+        s1((1, 0), 2)
+        p1((1, 0), 2)
+        s1((1, 0), 3)
+        p1((1, 0), 3)
+        s2((0, 0), 0)
+        qs((1, 1))
+        t((1, 0), 0)
+        qw((0, 1))
+        evt((1, 0), 0)
+        s2((0, 0), 1)
+        qw((1, 1))
+        s2((0, 0), 2)
+        fv((0, 0), 0)
+        s2((0, 0), 3)
+        st((0, 0), 0)
+        fv((0, 0), 1)
+        fe((0, 0), 3)
+        t((1, 0), 1)
+        fg((0, 0), 3)
+        st((0, 0), 1)
+        fv((0, 0), 2)
+        evt((1, 0), 1)
+        t((1, 0), 2)
+        st((0, 0), 2)
+        evt((1, 0), 2)
+        t((1, 0), 3)
+        st((0, 0), 3)
+        evt((1, 0), 3)
+        s2((0, 1), 0)
+        fv((0, 1), 0)
+        s2((0, 1), 1)
+        st((0, 1), 0)
+        qs((1, 0))
+        s2((0, 1), 2)
+        fv((0, 1), 1)
+        fe((0, 1), 2)
+        s2((0, 1), 3)
+        fg((0, 1), 2)
+        st((0, 1), 1)
+        fv((0, 1), 3)
+        s2((1, 0), 0)
+        st((0, 1), 3)
+        fv((1, 0), 0)
+        s2((1, 0), 1)
+        st((1, 0), 0)
+        fv((1, 0), 1)
+        s2((1, 0), 2)
+        st((0, 1), 2)
+        fe((1, 0), 2)
+        s2((1, 0), 3)
+        fg((1, 0), 2)
+        st((1, 0), 1)
+        fv((1, 0), 3)
+        s2((1, 1), 0)
+        st((1, 0), 3)
+        fv((1, 1), 0)
+        s2((1, 1), 1)
+        st((1, 1), 0)
+        fv((1, 1), 1)
+        s2((1, 1), 2)
+        st((1, 0), 2)
+        fv((1, 1), 2)
+        s2((1, 1), 3)
+        st((1, 1), 1)
+        fv((1, 1), 3)
+        st((1, 1), 2)
+        st((1, 1), 3)

@@ -55,13 +55,21 @@ def tile_graphconvolution_kernel(tc, prott5_emd, adj, h0, weight, lamda, alpha, 
             x_plane[u] = keep.tile([P, HALF], U8, name="xs" + tagn, align_bytes=64)
             h0_sb[u] = keep.tile([P, 4, HALF], BF16, name="h0" + tagn)
             r_sb[u] = keep.tile([P, 4, HALF], F32, name="r" + tagn)
-            sgr[u] = keep.tile([P, 4, P, 4], BF16, name="sgr" + tagn, align_bytes=64)
-            s_codes[u] = keep.tile([P, HALF], U32, name="sc" + tagn, align_bytes=64)
-            s_plane[u] = keep.tile([P, HALF], U8, name="ss" + tagn, align_bytes=64)
             wraw[u] = keep.tile([P, 4, HALF], BF16, name="wraw" + tagn)
-            wgr[u] = keep.tile([P, HALF, 4], BF16, name="wgr" + tagn, align_bytes=64)
-            w_codes[u] = keep.tile([P, HALF], U32, name="wc" + tagn, align_bytes=64)
-            w_plane[u] = keep.tile([P, HALF], U8, name="ws" + tagn, align_bytes=64)
+        s_all, w_all = {}, {}
+        for k in range(2):
+            sg = keep.tile([P, 2, 4, P, 4], BF16, name="sg%d" % k, align_bytes=64)
+            sc = keep.tile([P, 2 * HALF], U32, name="sc%d" % k, align_bytes=64)
+            ss = keep.tile([P, 2 * HALF], U8, name="ss%d" % k, align_bytes=64)
+            wg = keep.tile([P, 2, HALF, 4], BF16, name="wg%d" % k, align_bytes=64)
+            wc = keep.tile([P, 2 * HALF], U32, name="wc%d" % k, align_bytes=64)
+            ws = keep.tile([P, 2 * HALF], U8, name="ws%d" % k, align_bytes=64)
+            s_all[k] = (sc, ss, sg)
+            w_all[k] = (wc, ws, wg)
+            for c in range(2):
+                part = slice(HALF * c, HALF * c + HALF)
+                sgr[(k, c)], s_codes[(k, c)], s_plane[(k, c)] = sg[:, c], sc[:, part], ss[:, part]
+                wgr[(c, k)], w_codes[(c, k)], w_plane[(c, k)] = wg[:, c], wc[:, part], ws[:, part]
 
         adj_words = adj_sb[:].bitcast(F32).rearrange("p (i w u) -> p i w u", i=4, u=2)
         agr_words = agr[:].bitcast(F32).rearrange("p (n u) -> p n u", u=2)
@@ -136,10 +144,18 @@ def tile_graphconvolution_kernel(tc, prott5_emd, adj, h0, weight, lamda, alpha, 
             quant(x_codes[u], x_plane[u], xgr[u][:].rearrange("p w j -> p (w j)"))
 
         def qw(u):
-            quant(w_codes[u], w_plane[u], wgr[u][:].rearrange("p w j -> p (w j)"))
+            quant(w_codes[u], w_plane[u], wgr[u].rearrange("p w j -> p (w j)"))
+
+        def qS(b):
+            codes, plane, grouped = s_all[b]
+            quant(codes, plane, grouped[:].rearrange("p c i n j -> p (c i n j)"))
+
+        def qW(h):
+            codes, plane, grouped = w_all[h]
+            quant(codes, plane, grouped[:].rearrange("p c w j -> p (c w j)"))
 
         def qs(u):
-            quant(s_codes[u], s_plane[u], sgr[u][:].rearrange("p i n j -> p (i n j)"))
+            quant(s_codes[u], s_plane[u], sgr[u].rearrange("p i n j -> p (i n j)"))
 
         def ps(u, hp, eng):
             dst = r_sb[u][:, 2 * hp : 2 * hp + 2, :]
@@ -234,8 +250,12 @@ def tile_graphconvolution_kernel(tc, prott5_emd, adj, h0, weight, lamda, alpha, 
                 nc.gpsimd.tensor_copy(out=hold_sb[:], in_=x_codes[u][:, 0:1])
             elif what == "qs":
                 nc.gpsimd.tensor_copy(out=hold_sb[:], in_=s_codes[u][:, 0:1])
+            elif what == "qS":
+                nc.gpsimd.tensor_copy(out=hold_sb[:], in_=s_all[u][0][:, 0:1])
+            elif what == "qW":
+                nc.gpsimd.tensor_copy(out=hold_sb[:], in_=w_all[u][0][:, 0:1])
             else:
-                nc.gpsimd.tensor_copy(out=hold_sb[:], in_=wgr[u][:, 0:1, 0:2].bitcast(U32))
+                nc.gpsimd.tensor_copy(out=hold_sb[:], in_=wgr[u].rearrange("p w j -> p (w j)")[:, 0:2].bitcast(U32))
 
         def st(u, i):
             b, h = u
@@ -264,23 +284,23 @@ def tile_graphconvolution_kernel(tc, prott5_emd, adj, h0, weight, lamda, alpha, 
         ps((0, 0), 1, "s")
         s1((0, 0), 1)
         hold("qx", (0, 1))
-        ld("X10")
+        ld("h11")
         p1((0, 0), 0)
         rx((1, 1), "s")
         s1((0, 0), 2)
         ps((0, 1), 0, "g")
-        ld("h10")
+        ld("X10")
         p1((0, 0), 1)
         s1((0, 0), 3)
         ps((0, 1), 1, "g")
-        ld("h11")
+        ld("h10")
         p1((0, 0), 2)
         s1((0, 1), 0)
-        ps((1, 0), 0, "g")
+        ps((1, 1), 0, "g")
         ld("W10")
         p1((0, 0), 3)
         t((0, 0), 0)
-        ps((1, 0), 1, "g")
+        ps((1, 1), 1, "g")
         ld("W00")
         p1((0, 1), 0)
         evt((0, 0), 0)
@@ -296,18 +316,17 @@ def tile_graphconvolution_kernel(tc, prott5_emd, adj, h0, weight, lamda, alpha, 
         evt((0, 0), 2)
         s1((0, 1), 3)
         p1((0, 1), 3)
-        ps((1, 1), 0, "s")
         t((0, 0), 3)
         qx((1, 1))
-        ps((1, 1), 1, "s")
-        t((0, 1), 0)
-        rw((1, 0), "v")
         evt((0, 0), 3)
+        t((0, 1), 0)
+        hold("qx", (1, 1))
+        rx((1, 0), "s")
         t((0, 1), 1)
-        hold("rw", (1, 0))
+        ps((1, 0), 0, "g")
         evt((0, 1), 0)
         t((0, 1), 2)
-        rx((1, 0), "g")
+        ps((1, 0), 1, "g")
         evt((0, 1), 1)
         s1((1, 1), 0)
         p1((1, 1), 0)
@@ -319,26 +338,25 @@ def tile_graphconvolution_kernel(tc, prott5_emd, adj, h0, weight, lamda, alpha, 
         s1((1, 1), 3)
         p1((1, 1), 3)
         t((0, 1), 3)
-        qs((0, 0))
+        rw((1, 0), "v")
         evt((0, 1), 3)
         t((1, 1), 0)
-        qs((0, 1))
+        qS(0)
         rw((0, 0), "s")
         t((1, 1), 1)
         qx((1, 0))
         evt((1, 1), 0)
         t((1, 1), 2)
-        qw((1, 0))
+        qW(0)
         evt((1, 1), 1)
         t((1, 1), 3)
-        qw((0, 0))
+        hold("qW", 0)
         evt((1, 1), 2)
         s1((1, 0), 0)
-        hold("qw", (0, 0))
+        rw((0, 1), "g")
         p1((1, 0), 0)
         evt((1, 1), 3)
         s1((1, 0), 1)
-        rw((0, 1), "g")
         p1((1, 0), 1)
         rw((1, 1), "s")
         s1((1, 0), 2)
@@ -346,35 +364,32 @@ def tile_graphconvolution_kernel(tc, prott5_emd, adj, h0, weight, lamda, alpha, 
         s1((1, 0), 3)
         p1((1, 0), 3)
         s2((0, 0), 0)
-        qs((1, 1))
+        fv((0, 0), 0)
         t((1, 0), 0)
-        qw((0, 1))
+        st((0, 0), 0)
         evt((1, 0), 0)
         s2((0, 0), 1)
-        qw((1, 1))
-        s2((0, 0), 2)
-        fv((0, 0), 0)
-        s2((0, 0), 3)
-        st((0, 0), 0)
         fv((0, 0), 1)
-        fe((0, 0), 3)
-        t((1, 0), 1)
-        fg((0, 0), 3)
+        s2((0, 0), 2)
         st((0, 0), 1)
         fv((0, 0), 2)
+        s2((0, 0), 3)
+        st((0, 0), 2)
+        fv((0, 0), 3)
+        t((1, 0), 1)
+        st((0, 0), 3)
+        qW(1)
         evt((1, 0), 1)
         t((1, 0), 2)
-        st((0, 0), 2)
         evt((1, 0), 2)
         t((1, 0), 3)
-        st((0, 0), 3)
         evt((1, 0), 3)
         s2((0, 1), 0)
-        fv((0, 1), 0)
+        qS(1)
         s2((0, 1), 1)
-        st((0, 1), 0)
-        qs((1, 0))
+        fv((0, 1), 0)
         s2((0, 1), 2)
+        st((0, 1), 0)
         fv((0, 1), 1)
         fe((0, 1), 2)
         s2((0, 1), 3)

@@ -17,7 +17,7 @@ COPY = mybir.ActivationFunctionType.Copy
 
 P = 128
 HALF = 512
-LATE = ()
+LATE = ((0, 1), (1, 1), (1, 0),)
 
 
 def tile_graphconvolution_kernel(tc, prott5_emd, adj, h0, weight, lamda, alpha, l, out):
@@ -38,6 +38,8 @@ def tile_graphconvolution_kernel(tc, prott5_emd, adj, h0, weight, lamda, alpha, 
 
         ident = keep.tile([P, P], F32, name="ident")
         make_identity(nc, ident[:])
+        warm_sb = keep.tile([P, HALF], BF16, name="warm_sb")
+        nc.vector.memset(warm_sb[:], 0.0)
 
         adj_sb = keep.tile([P, 4 * 512], BF16, name="adj_sb")
         agr = keep.tile([P, 2048], BF16, name="agr", align_bytes=64)
@@ -73,8 +75,8 @@ def tile_graphconvolution_kernel(tc, prott5_emd, adj, h0, weight, lamda, alpha, 
 
         adj_words = adj_sb[:].bitcast(F32).rearrange("p (i w u) -> p i w u", i=4, u=2)
         agr_words = agr[:].bitcast(F32).rearrange("p (n u) -> p n u", u=2)
-        hold_sb = keep.tile([P, 1], U32, name="hold_sb")
         live = {}
+        banks = []
 
         def ld(name):
             if name == "adj":
@@ -167,8 +169,21 @@ def tile_graphconvolution_kernel(tc, prott5_emd, adj, h0, weight, lamda, alpha, 
             else:
                 nc.scalar.activation(out=dst, in_=src, func=COPY, scale=h0_gain)
 
+        def next_bank():
+            bank = live.pop("next", None)
+            if bank is None:
+                bank = accp.tile([P, HALF], F32, name="bank%d" % len(banks), tag="acc")
+                banks.append(bank)
+            return bank
+
+        def wa(count):
+            bank = next_bank()
+            live["next"] = bank
+            for k in range(count):
+                nc.tensor.matmul(bank[:], warm_sb[:, 0:P], warm_sb[:], start=True, stop=True)
+
         def s1(u, i):
-            a = accp.tile([P, HALF], F32, name="acc1_%d%d%d" % (u[0], u[1], i), tag="acc")
+            a = next_bank()
             live[(1, u, i)] = a
             nc.tensor.matmul_mx(
                 out=a[:],
@@ -215,7 +230,7 @@ def tile_graphconvolution_kernel(tc, prott5_emd, adj, h0, weight, lamda, alpha, 
 
         def s2(u, i):
             b, h = u
-            a = accp.tile([P, HALF], F32, name="acc2_%d%d%d" % (b, h, i), tag="acc")
+            a = next_bank()
             live[(2, u, i)] = a
             for c in range(2):
                 nc.tensor.matmul_mx(
@@ -241,22 +256,6 @@ def tile_graphconvolution_kernel(tc, prott5_emd, adj, h0, weight, lamda, alpha, 
         def fg(u, i):
             nc.gpsimd.tensor_tensor(out=r_sb[u][:, i, :], in0=live[("u", u, i)][:], in1=r_sb[u][:, i, :], op=ADD)
 
-        def hold(what, u, i=0):
-            if what == "p1":
-                nc.gpsimd.tensor_copy(out=hold_sb[:].bitcast(F32), in_=r_sb[u][:, i, 0:1])
-            elif what == "qw":
-                nc.gpsimd.tensor_copy(out=hold_sb[:], in_=w_codes[u][:, 0:1])
-            elif what == "qx":
-                nc.gpsimd.tensor_copy(out=hold_sb[:], in_=x_codes[u][:, 0:1])
-            elif what == "qs":
-                nc.gpsimd.tensor_copy(out=hold_sb[:], in_=s_codes[u][:, 0:1])
-            elif what == "qS":
-                nc.gpsimd.tensor_copy(out=hold_sb[:], in_=s_all[u][0][:, 0:1])
-            elif what == "qW":
-                nc.gpsimd.tensor_copy(out=hold_sb[:], in_=w_all[u][0][:, 0:1])
-            else:
-                nc.gpsimd.tensor_copy(out=hold_sb[:], in_=wgr[u].rearrange("p w j -> p (w j)")[:, 0:2].bitcast(U32))
-
         def st(u, i):
             b, h = u
             nc.sync.dma_start(
@@ -273,153 +272,158 @@ def tile_graphconvolution_kernel(tc, prott5_emd, adj, h0, weight, lamda, alpha, 
         rx((0, 1), "v")
         eva(0, "s")
         ta(1)
-        ld("h00")
+        ld("X10")
         eva(1, "s")
-        ld("h01")
-        qa()
-        ps((0, 0), 0, "s")
-        s1((0, 0), 0)
+        wa(4)
         ld("X11")
+        qa()
+        rx((1, 0), "s")
+        s1((0, 0), 0)
+        ld("h00")
         qx((0, 1))
-        ps((0, 0), 1, "s")
+        ps((0, 0), 0, "s")
         s1((0, 0), 1)
-        hold("qx", (0, 1))
+        ld("h01")
+        rx((1, 1), "v")
+        ps((0, 0), 1, "s")
+        s1((0, 0), 2)
+        ld("W10")
+        qx((1, 0))
+        wa(6)
+        rw((1, 0), "g")
+        ld("W00")
+        qx((1, 1))
+        s1((0, 0), 3)
+        rw((0, 0), "g")
         ld("h11")
         p1((0, 0), 0)
-        rx((1, 1), "s")
-        s1((0, 0), 2)
-        ps((0, 1), 0, "g")
-        ld("X10")
-        p1((0, 0), 1)
-        s1((0, 0), 3)
-        ps((0, 1), 1, "g")
-        ld("h10")
-        p1((0, 0), 2)
         s1((0, 1), 0)
-        ps((1, 1), 0, "g")
-        ld("W10")
-        p1((0, 0), 3)
-        t((0, 0), 0)
-        ps((1, 1), 1, "g")
-        ld("W00")
-        p1((0, 1), 0)
-        evt((0, 0), 0)
+        ld("h10")
+        p1((0, 0), 1)
         s1((0, 1), 1)
         ld("W01")
-        p1((0, 1), 1)
-        t((0, 0), 1)
+        p1((0, 0), 2)
+        t((0, 0), 0)
+        rw((0, 1), "g")
         ld("W11")
+        p1((0, 0), 3)
+        evt((0, 0), 0)
+        t((0, 0), 1)
+        p1((0, 1), 0)
         evt((0, 0), 1)
         s1((0, 1), 2)
+        p1((0, 1), 1)
+        s1((0, 1), 3)
         p1((0, 1), 2)
         t((0, 0), 2)
-        evt((0, 0), 2)
-        s1((0, 1), 3)
         p1((0, 1), 3)
+        evt((0, 0), 2)
         t((0, 0), 3)
-        qx((1, 1))
         evt((0, 0), 3)
-        t((0, 1), 0)
-        hold("qx", (1, 1))
-        rx((1, 0), "s")
-        t((0, 1), 1)
-        ps((1, 0), 0, "g")
-        evt((0, 1), 0)
-        t((0, 1), 2)
-        ps((1, 0), 1, "g")
-        evt((0, 1), 1)
         s1((1, 1), 0)
         p1((1, 1), 0)
-        evt((0, 1), 2)
         s1((1, 1), 1)
         p1((1, 1), 1)
+        t((0, 1), 0)
+        evt((0, 1), 0)
+        t((0, 1), 1)
+        evt((0, 1), 1)
         s1((1, 1), 2)
         p1((1, 1), 2)
         s1((1, 1), 3)
         p1((1, 1), 3)
+        t((0, 1), 2)
+        evt((0, 1), 2)
         t((0, 1), 3)
-        rw((1, 0), "v")
         evt((0, 1), 3)
-        t((1, 1), 0)
-        qS(0)
-        rw((0, 0), "s")
-        t((1, 1), 1)
-        qx((1, 0))
-        evt((1, 1), 0)
-        t((1, 1), 2)
-        qW(0)
-        evt((1, 1), 1)
-        t((1, 1), 3)
-        hold("qW", 0)
-        evt((1, 1), 2)
         s1((1, 0), 0)
-        rw((0, 1), "g")
         p1((1, 0), 0)
-        evt((1, 1), 3)
+        rw((1, 1), "s")
         s1((1, 0), 1)
         p1((1, 0), 1)
-        rw((1, 1), "s")
         s1((1, 0), 2)
         p1((1, 0), 2)
         s1((1, 0), 3)
         p1((1, 0), 3)
+        t((1, 1), 0)
+        qS(0)
+        evt((1, 1), 0)
+        t((1, 1), 1)
+        qW(0)
+        evt((1, 1), 1)
+        wa(2)
+        qW(1)
+        t((1, 1), 2)
+        evt((1, 1), 2)
+        wa(1)
+        t((1, 1), 3)
+        evt((1, 1), 3)
+        wa(1)
+        t((1, 0), 0)
+        evt((1, 0), 0)
+        wa(1)
+        t((1, 0), 1)
+        evt((1, 0), 1)
+        wa(1)
+        t((1, 0), 2)
+        evt((1, 0), 2)
+        wa(1)
+        t((1, 0), 3)
+        evt((1, 0), 3)
         s2((0, 0), 0)
         fv((0, 0), 0)
-        t((1, 0), 0)
-        st((0, 0), 0)
-        evt((1, 0), 0)
+        rs((0, 1), 0, "s")
         s2((0, 0), 1)
+        st((0, 0), 0)
         fv((0, 0), 1)
+        rs((0, 1), 1, "s")
         s2((0, 0), 2)
         st((0, 0), 1)
         fv((0, 0), 2)
+        rs((1, 0), 0, "s")
         s2((0, 0), 3)
         st((0, 0), 2)
         fv((0, 0), 3)
-        t((1, 0), 1)
-        st((0, 0), 3)
-        qW(1)
-        evt((1, 0), 1)
-        t((1, 0), 2)
-        evt((1, 0), 2)
-        t((1, 0), 3)
-        evt((1, 0), 3)
+        rs((1, 0), 1, "s")
         s2((0, 1), 0)
+        st((0, 0), 3)
         qS(1)
+        rs((1, 1), 0, "s")
         s2((0, 1), 1)
         fv((0, 1), 0)
+        rs((1, 1), 1, "s")
         s2((0, 1), 2)
         st((0, 1), 0)
         fv((0, 1), 1)
-        fe((0, 1), 2)
         s2((0, 1), 3)
-        fg((0, 1), 2)
         st((0, 1), 1)
-        fv((0, 1), 3)
+        fv((0, 1), 2)
         s2((1, 0), 0)
+        st((0, 1), 2)
+        fv((0, 1), 3)
+        s2((1, 0), 1)
         st((0, 1), 3)
         fv((1, 0), 0)
-        s2((1, 0), 1)
-        st((1, 0), 0)
-        fv((1, 0), 1)
+        fe((1, 0), 1)
         s2((1, 0), 2)
-        st((0, 1), 2)
-        fe((1, 0), 2)
+        fg((1, 0), 1)
+        st((1, 0), 0)
+        fv((1, 0), 2)
         s2((1, 0), 3)
-        fg((1, 0), 2)
-        st((1, 0), 1)
+        st((1, 0), 2)
         fv((1, 0), 3)
         s2((1, 1), 0)
         st((1, 0), 3)
-        fv((1, 1), 0)
+        fe((1, 1), 0)
         s2((1, 1), 1)
-        st((1, 1), 0)
+        fg((1, 1), 0)
+        st((1, 0), 1)
         fv((1, 1), 1)
         s2((1, 1), 2)
-        st((1, 0), 2)
+        st((1, 1), 1)
         fv((1, 1), 2)
         s2((1, 1), 3)
-        st((1, 1), 1)
-        fv((1, 1), 3)
         st((1, 1), 2)
+        fv((1, 1), 3)
         st((1, 1), 3)
+        st((1, 1), 0)

@@ -17,7 +17,7 @@ COPY = mybir.ActivationFunctionType.Copy
 
 P = 128
 HALF = 512
-LATE = ((0, 1), (1, 1), (1, 0),)
+LATE = ((0, 1), (1, 0), (1, 1),)
 
 
 def tile_graphconvolution_kernel(tc, prott5_emd, adj, h0, weight, lamda, alpha, l, out):
@@ -52,13 +52,10 @@ def tile_graphconvolution_kernel(tc, prott5_emd, adj, h0, weight, lamda, alpha, 
         for u in units:
             tagn = "%d%d" % u
             xraw[u] = keep.tile([P, 4, HALF], BF16, name="xraw" + tagn)
-            xgr[u] = keep.tile([P, HALF, 4], BF16, name="xgr" + tagn, align_bytes=64)
-            x_codes[u] = keep.tile([P, HALF], U32, name="xc" + tagn, align_bytes=64)
-            x_plane[u] = keep.tile([P, HALF], U8, name="xs" + tagn, align_bytes=64)
             h0_sb[u] = keep.tile([P, 4, HALF], BF16, name="h0" + tagn)
             r_sb[u] = keep.tile([P, 4, HALF], F32, name="r" + tagn)
             wraw[u] = keep.tile([P, 4, HALF], BF16, name="wraw" + tagn)
-        s_all, w_all = {}, {}
+        s_all, w_all, x_all = {}, {}, {}
         for k in range(2):
             sg = keep.tile([P, 2, 4, P, 4], BF16, name="sg%d" % k, align_bytes=64)
             sc = keep.tile([P, 2 * HALF], U32, name="sc%d" % k, align_bytes=64)
@@ -66,11 +63,16 @@ def tile_graphconvolution_kernel(tc, prott5_emd, adj, h0, weight, lamda, alpha, 
             wg = keep.tile([P, 2, HALF, 4], BF16, name="wg%d" % k, align_bytes=64)
             wc = keep.tile([P, 2 * HALF], U32, name="wc%d" % k, align_bytes=64)
             ws = keep.tile([P, 2 * HALF], U8, name="ws%d" % k, align_bytes=64)
+            xg = keep.tile([P, 2, HALF, 4], BF16, name="xg%d" % k, align_bytes=64)
+            xc = keep.tile([P, 2 * HALF], U32, name="xc%d" % k, align_bytes=64)
+            xs = keep.tile([P, 2 * HALF], U8, name="xs%d" % k, align_bytes=64)
+            x_all[k] = (xc, xs, xg)
             s_all[k] = (sc, ss, sg)
             w_all[k] = (wc, ws, wg)
             for c in range(2):
                 part = slice(HALF * c, HALF * c + HALF)
                 sgr[(k, c)], s_codes[(k, c)], s_plane[(k, c)] = sg[:, c], sc[:, part], ss[:, part]
+                xgr[(k, c)], x_codes[(k, c)], x_plane[(k, c)] = xg[:, c], xc[:, part], xs[:, part]
                 wgr[(c, k)], w_codes[(c, k)], w_plane[(c, k)] = wg[:, c], wc[:, part], ws[:, part]
 
         adj_words = adj_sb[:].bitcast(F32).rearrange("p (i w u) -> p i w u", i=4, u=2)
@@ -143,7 +145,7 @@ def tile_graphconvolution_kernel(tc, prott5_emd, adj, h0, weight, lamda, alpha, 
             regroup(eng, wgr[u], wraw[u])
 
         def qx(u):
-            quant(x_codes[u], x_plane[u], xgr[u][:].rearrange("p w j -> p (w j)"))
+            quant(x_codes[u], x_plane[u], xgr[u].rearrange("p w j -> p (w j)"))
 
         def qw(u):
             quant(w_codes[u], w_plane[u], wgr[u].rearrange("p w j -> p (w j)"))
@@ -151,6 +153,10 @@ def tile_graphconvolution_kernel(tc, prott5_emd, adj, h0, weight, lamda, alpha, 
         def qS(b):
             codes, plane, grouped = s_all[b]
             quant(codes, plane, grouped[:].rearrange("p c i n j -> p (c i n j)"))
+
+        def qX(b):
+            codes, plane, grouped = x_all[b]
+            quant(codes, plane, grouped[:].rearrange("p h w j -> p (h w j)"))
 
         def qW(h):
             codes, plane, grouped = w_all[h]
@@ -181,6 +187,21 @@ def tile_graphconvolution_kernel(tc, prott5_emd, adj, h0, weight, lamda, alpha, 
             live["next"] = bank
             for k in range(count):
                 nc.tensor.matmul(bank[:], warm_sb[:, 0:P], warm_sb[:], start=True, stop=True)
+
+        def wx(count):
+            bank = next_bank()
+            live["next"] = bank
+            codes, plane = x_codes[(0, 0)], x_plane[(0, 0)]
+            for k in range(count):
+                nc.tensor.matmul_mx(
+                    out=bank[:],
+                    lhsT=codes[:, 0:P].bitcast(FP8X4),
+                    lhsT_scale=plane[:, 0:P],
+                    rhs=codes[:].bitcast(FP8X4),
+                    rhs_scale=plane[:],
+                    start=True,
+                    stop=True,
+                )
 
         def s1(u, i):
             a = next_bank()
@@ -256,6 +277,16 @@ def tile_graphconvolution_kernel(tc, prott5_emd, adj, h0, weight, lamda, alpha, 
         def fg(u, i):
             nc.gpsimd.tensor_tensor(out=r_sb[u][:, i, :], in0=live[("u", u, i)][:], in1=r_sb[u][:, i, :], op=ADD)
 
+        def hold(what, u, i=0):
+            if what == "qS":
+                nc.gpsimd.memset(s_all[u][2][:, 0, 0, 0, 0:2], 0.0)
+            elif what == "qW":
+                nc.gpsimd.memset(w_all[u][2][:, 0, 0, 0:2], 0.0)
+            elif what == "qx":
+                nc.gpsimd.memset(xgr[u][:, 0, 0:2], 0.0)
+            elif what == "rw":
+                nc.gpsimd.memset(wraw[u][:, 0, 0:2], 0.0)
+
         def st(u, i):
             b, h = u
             nc.sync.dma_start(
@@ -265,6 +296,7 @@ def tile_graphconvolution_kernel(tc, prott5_emd, adj, h0, weight, lamda, alpha, 
 
         ld("X00")
         rx((0, 0), "v")
+        wa(6)
         ld("adj")
         qx((0, 0))
         ta(0)
@@ -272,152 +304,152 @@ def tile_graphconvolution_kernel(tc, prott5_emd, adj, h0, weight, lamda, alpha, 
         rx((0, 1), "v")
         eva(0, "s")
         ta(1)
-        ld("X10")
-        eva(1, "s")
-        wa(4)
-        ld("X11")
-        qa()
-        rx((1, 0), "s")
-        s1((0, 0), 0)
         ld("h00")
-        qx((0, 1))
+        eva(1, "s")
+        wx(4)
+        ld("X10")
+        qa()
         ps((0, 0), 0, "s")
+        s1((0, 0), 0)
+        rx((1, 0), "g")
+        ld("X11")
+        qx((0, 1))
+        ps((0, 0), 1, "s")
         s1((0, 0), 1)
         ld("h01")
-        rx((1, 1), "v")
-        ps((0, 0), 1, "s")
+        p1((0, 0), 0)
+        rx((1, 1), "s")
         s1((0, 0), 2)
         ld("W10")
-        qx((1, 0))
-        wa(6)
-        rw((1, 0), "g")
-        ld("W00")
-        qx((1, 1))
-        s1((0, 0), 3)
-        rw((0, 0), "g")
-        ld("h11")
-        p1((0, 0), 0)
-        s1((0, 1), 0)
-        ld("h10")
         p1((0, 0), 1)
-        s1((0, 1), 1)
-        ld("W01")
+        s1((0, 0), 3)
+        rw((1, 0), "g")
+        ld("h10")
         p1((0, 0), 2)
-        t((0, 0), 0)
-        rw((0, 1), "g")
-        ld("W11")
+        wx(1)
+        ld("W00")
         p1((0, 0), 3)
+        s1((0, 1), 0)
+        rw((0, 0), "g")
+        ld("W11")
+        qx((1, 0))
+        s1((0, 1), 1)
+        ld("h11")
+        qx((1, 1))
+        t((0, 0), 0)
+        ld("W01")
+        p1((0, 1), 0)
         evt((0, 0), 0)
         t((0, 0), 1)
-        p1((0, 1), 0)
-        evt((0, 0), 1)
-        s1((0, 1), 2)
         p1((0, 1), 1)
-        s1((0, 1), 3)
-        p1((0, 1), 2)
+        evt((0, 0), 1)
         t((0, 0), 2)
-        p1((0, 1), 3)
         evt((0, 0), 2)
         t((0, 0), 3)
         evt((0, 0), 3)
-        s1((1, 1), 0)
-        p1((1, 1), 0)
-        s1((1, 1), 1)
-        p1((1, 1), 1)
+        wx(2)
+        s1((0, 1), 2)
+        p1((0, 1), 2)
+        s1((0, 1), 3)
+        p1((0, 1), 3)
+        s1((1, 0), 0)
+        p1((1, 0), 0)
         t((0, 1), 0)
         evt((0, 1), 0)
         t((0, 1), 1)
+        rs((0, 1), 0, "g")
         evt((0, 1), 1)
-        s1((1, 1), 2)
-        p1((1, 1), 2)
-        s1((1, 1), 3)
-        p1((1, 1), 3)
-        t((0, 1), 2)
-        evt((0, 1), 2)
-        t((0, 1), 3)
-        evt((0, 1), 3)
-        s1((1, 0), 0)
-        p1((1, 0), 0)
-        rw((1, 1), "s")
         s1((1, 0), 1)
         p1((1, 0), 1)
         s1((1, 0), 2)
         p1((1, 0), 2)
+        t((0, 1), 2)
+        evt((0, 1), 2)
+        t((0, 1), 3)
+        evt((0, 1), 3)
         s1((1, 0), 3)
         p1((1, 0), 3)
-        t((1, 1), 0)
-        qS(0)
-        evt((1, 1), 0)
-        t((1, 1), 1)
-        qW(0)
-        evt((1, 1), 1)
-        wa(2)
-        qW(1)
-        t((1, 1), 2)
-        evt((1, 1), 2)
-        wa(1)
-        t((1, 1), 3)
-        evt((1, 1), 3)
-        wa(1)
+        s1((1, 1), 0)
+        p1((1, 1), 0)
         t((1, 0), 0)
         evt((1, 0), 0)
-        wa(1)
         t((1, 0), 1)
         evt((1, 0), 1)
-        wa(1)
+        s1((1, 1), 1)
+        p1((1, 1), 1)
+        s1((1, 1), 2)
+        p1((1, 1), 2)
         t((1, 0), 2)
         evt((1, 0), 2)
-        wa(1)
         t((1, 0), 3)
         evt((1, 0), 3)
+        s1((1, 1), 3)
+        p1((1, 1), 3)
+        wx(2)
+        qS(0)
+        t((1, 1), 0)
+        qW(0)
+        evt((1, 1), 0)
+        t((1, 1), 1)
+        evt((1, 1), 1)
+        t((1, 1), 2)
+        evt((1, 1), 2)
+        t((1, 1), 3)
+        evt((1, 1), 3)
+        wx(2)
+        qS(1)
+        rw((1, 1), "s")
         s2((0, 0), 0)
+        hold("qS", 1)
         fv((0, 0), 0)
-        rs((0, 1), 0, "s")
+        rw((0, 1), "s")
         s2((0, 0), 1)
+        rs((1, 0), 0, "g")
         st((0, 0), 0)
         fv((0, 0), 1)
         rs((0, 1), 1, "s")
         s2((0, 0), 2)
+        rs((1, 0), 1, "g")
         st((0, 0), 1)
         fv((0, 0), 2)
-        rs((1, 0), 0, "s")
         s2((0, 0), 3)
         st((0, 0), 2)
         fv((0, 0), 3)
-        rs((1, 0), 1, "s")
-        s2((0, 1), 0)
-        st((0, 0), 3)
-        qS(1)
-        rs((1, 1), 0, "s")
-        s2((0, 1), 1)
-        fv((0, 1), 0)
-        rs((1, 1), 1, "s")
-        s2((0, 1), 2)
-        st((0, 1), 0)
-        fv((0, 1), 1)
-        s2((0, 1), 3)
-        st((0, 1), 1)
-        fv((0, 1), 2)
         s2((1, 0), 0)
+        st((0, 0), 3)
+        fv((1, 0), 0)
+        s2((1, 0), 1)
+        st((1, 0), 0)
+        qW(1)
+        s2((1, 0), 2)
+        fv((1, 0), 1)
+        s2((1, 0), 3)
+        st((1, 0), 1)
+        fv((1, 0), 2)
+        fe((1, 0), 3)
+        wx(1)
+        fg((1, 0), 3)
+        st((1, 0), 2)
+        rs((1, 1), 0, "s")
+        s2((0, 1), 0)
+        fv((0, 1), 0)
+        s2((0, 1), 1)
+        st((0, 1), 0)
+        fe((0, 1), 1)
+        s2((0, 1), 2)
+        fg((0, 1), 1)
+        st((1, 0), 3)
+        fv((0, 1), 2)
+        rs((1, 1), 1, "s")
+        s2((0, 1), 3)
         st((0, 1), 2)
         fv((0, 1), 3)
-        s2((1, 0), 1)
-        st((0, 1), 3)
-        fv((1, 0), 0)
-        fe((1, 0), 1)
-        s2((1, 0), 2)
-        fg((1, 0), 1)
-        st((1, 0), 0)
-        fv((1, 0), 2)
-        s2((1, 0), 3)
-        st((1, 0), 2)
-        fv((1, 0), 3)
         s2((1, 1), 0)
-        st((1, 0), 3)
+        st((0, 1), 3)
         fe((1, 1), 0)
         s2((1, 1), 1)
         fg((1, 1), 0)
-        st((1, 0), 1)
+        st((0, 1), 1)
         fv((1, 1), 1)
         s2((1, 1), 2)
         st((1, 1), 1)
@@ -425,5 +457,5 @@ def tile_graphconvolution_kernel(tc, prott5_emd, adj, h0, weight, lamda, alpha, 
         s2((1, 1), 3)
         st((1, 1), 2)
         fv((1, 1), 3)
-        st((1, 1), 3)
         st((1, 1), 0)
+        st((1, 1), 3)

@@ -51,12 +51,13 @@ def tile_graphconvolution_kernel(tc, prott5_emd, adj, h0, weight, lamda, alpha, 
         wraw, wgr, w_codes, w_plane = {}, {}, {}, {}
         for u in units:
             tagn = "%d%d" % u
-            xraw[u] = keep.tile([P, 4, HALF], BF16, name="xraw" + tagn)
-            h0_sb[u] = keep.tile([P, 4, HALF], BF16, name="h0" + tagn)
             r_sb[u] = keep.tile([P, 4, HALF], F32, name="r" + tagn)
-            wraw[u] = keep.tile([P, 4, HALF], BF16, name="wraw" + tagn)
         s_all, w_all, x_all = {}, {}, {}
+        x_in, h0_in, w_in = {}, {}, {}
         for k in range(2):
+            x_in[k] = keep.tile([P, 4, 2 * HALF], BF16, name="xin%d" % k)
+            h0_in[k] = keep.tile([P, 4, 2 * HALF], BF16, name="h0in%d" % k)
+            w_in[k] = keep.tile([P, 4, 2 * HALF], BF16, name="win%d" % k)
             sg = keep.tile([P, 2, 4, P, 4], BF16, name="sg%d" % k, align_bytes=64)
             sc = keep.tile([P, 2 * HALF], U32, name="sc%d" % k, align_bytes=64)
             ss = keep.tile([P, 2 * HALF], U8, name="ss%d" % k, align_bytes=64)
@@ -71,6 +72,7 @@ def tile_graphconvolution_kernel(tc, prott5_emd, adj, h0, weight, lamda, alpha, 
             w_all[k] = (wc, ws, wg)
             for c in range(2):
                 part = slice(HALF * c, HALF * c + HALF)
+                xraw[(k, c)], h0_sb[(k, c)], wraw[(k, c)] = x_in[k][:, :, part], h0_in[k][:, :, part], w_in[k][:, :, part]
                 sgr[(k, c)], s_codes[(k, c)], s_plane[(k, c)] = sg[:, c], sc[:, part], ss[:, part]
                 xgr[(k, c)], x_codes[(k, c)], x_plane[(k, c)] = xg[:, c], xc[:, part], xs[:, part]
                 wgr[(c, k)], w_codes[(c, k)], w_plane[(c, k)] = wg[:, c], wc[:, part], ws[:, part]
@@ -85,19 +87,16 @@ def tile_graphconvolution_kernel(tc, prott5_emd, adj, h0, weight, lamda, alpha, 
                 nc.sync.dma_start(out=adj_sb[:], in_=adj.rearrange("(p i) m -> p (i m)", i=4))
                 return
             a = int(name[1])
-            h = int(name[2])
-            cols = slice(HALF * h, HALF * h + HALF)
+            cols = slice(0, 2 * HALF) if len(name) == 2 else slice(HALF * int(name[2]), HALF * int(name[2]) + HALF)
             if name[0] == "X":
                 nc.sync.dma_start(
-                    out=xraw[(a, h)][:], in_=prott5_emd[a].rearrange("(p j) f -> p j f", j=4)[:, :, cols]
+                    out=x_in[a][:, :, cols], in_=prott5_emd[a].rearrange("(p j) f -> p j f", j=4)[:, :, cols]
                 )
             elif name[0] == "h":
-                nc.sync.dma_start(
-                    out=h0_sb[(a, h)][:], in_=h0[a].rearrange("(p i) f -> p i f", i=4)[:, :, cols]
-                )
+                nc.sync.dma_start(out=h0_in[a][:, :, cols], in_=h0[a].rearrange("(p i) f -> p i f", i=4)[:, :, cols])
             else:
                 nc.sync.dma_start(
-                    out=wraw[(a, h)][:],
+                    out=w_in[a][:, :, cols],
                     in_=weight[HALF * a : HALF * a + HALF, cols].rearrange("(j p) o -> p j o", p=P),
                 )
 
@@ -296,7 +295,7 @@ def tile_graphconvolution_kernel(tc, prott5_emd, adj, h0, weight, lamda, alpha, 
 
         ld("X00")
         rx((0, 0), "v")
-        wa(6)
+        wa(7)
         ld("adj")
         qx((0, 0))
         ta(0)
@@ -307,58 +306,55 @@ def tile_graphconvolution_kernel(tc, prott5_emd, adj, h0, weight, lamda, alpha, 
         ld("h00")
         eva(1, "s")
         wx(4)
-        ld("X10")
+        ld("X1")
         qa()
         ps((0, 0), 0, "s")
         s1((0, 0), 0)
         rx((1, 0), "g")
-        ld("X11")
+        ld("h01")
         qx((0, 1))
         ps((0, 0), 1, "s")
         s1((0, 0), 1)
-        ld("h01")
-        p1((0, 0), 0)
-        rx((1, 1), "s")
-        s1((0, 0), 2)
         ld("W10")
+        p1((0, 0), 0)
+        s1((0, 0), 2)
+        ld("h1")
         p1((0, 0), 1)
         s1((0, 0), 3)
-        rw((1, 0), "g")
-        ld("h10")
-        p1((0, 0), 2)
-        wx(1)
         ld("W00")
-        p1((0, 0), 3)
-        s1((0, 1), 0)
-        rw((0, 0), "g")
-        ld("W11")
-        qx((1, 0))
-        s1((0, 1), 1)
-        ld("h11")
-        qx((1, 1))
+        p1((0, 0), 2)
         t((0, 0), 0)
+        ld("W11")
+        p1((0, 0), 3)
+        evt((0, 0), 0)
+        s1((0, 1), 0)
         ld("W01")
         p1((0, 1), 0)
-        evt((0, 0), 0)
+        rx((1, 1), "s")
         t((0, 0), 1)
-        p1((0, 1), 1)
         evt((0, 0), 1)
+        s1((0, 1), 1)
+        p1((0, 1), 1)
+        s1((0, 1), 2)
+        qx((1, 0))
         t((0, 0), 2)
+        qx((1, 1))
         evt((0, 0), 2)
         t((0, 0), 3)
-        evt((0, 0), 3)
-        wx(2)
-        s1((0, 1), 2)
+        hold("qx", (1, 1))
         p1((0, 1), 2)
+        evt((0, 0), 3)
         s1((0, 1), 3)
+        rw((1, 0), "g")
         p1((0, 1), 3)
-        s1((1, 0), 0)
-        p1((1, 0), 0)
+        wx(3)
+        rw((0, 0), "g")
         t((0, 1), 0)
         evt((0, 1), 0)
         t((0, 1), 1)
-        rs((0, 1), 0, "g")
         evt((0, 1), 1)
+        s1((1, 0), 0)
+        p1((1, 0), 0)
         s1((1, 0), 1)
         p1((1, 0), 1)
         s1((1, 0), 2)
@@ -385,31 +381,31 @@ def tile_graphconvolution_kernel(tc, prott5_emd, adj, h0, weight, lamda, alpha, 
         evt((1, 0), 3)
         s1((1, 1), 3)
         p1((1, 1), 3)
-        wx(2)
+        wx(1)
         qS(0)
         t((1, 1), 0)
         qW(0)
         evt((1, 1), 0)
         t((1, 1), 1)
         evt((1, 1), 1)
+        wx(1)
         t((1, 1), 2)
         evt((1, 1), 2)
         t((1, 1), 3)
         evt((1, 1), 3)
-        wx(2)
+        wx(3)
         qS(1)
         rw((1, 1), "s")
         s2((0, 0), 0)
         hold("qS", 1)
         fv((0, 0), 0)
-        rw((0, 1), "s")
+        rs((1, 0), 0, "s")
         s2((0, 0), 1)
-        rs((1, 0), 0, "g")
+        rw((0, 1), "g")
         st((0, 0), 0)
         fv((0, 0), 1)
-        rs((0, 1), 1, "s")
+        rs((1, 0), 1, "s")
         s2((0, 0), 2)
-        rs((1, 0), 1, "g")
         st((0, 0), 1)
         fv((0, 0), 2)
         s2((0, 0), 3)
@@ -422,17 +418,20 @@ def tile_graphconvolution_kernel(tc, prott5_emd, adj, h0, weight, lamda, alpha, 
         st((1, 0), 0)
         qW(1)
         s2((1, 0), 2)
+        hold("qW", 1)
         fv((1, 0), 1)
         s2((1, 0), 3)
         st((1, 0), 1)
         fv((1, 0), 2)
         fe((1, 0), 3)
-        wx(1)
+        wx(4)
         fg((1, 0), 3)
         st((1, 0), 2)
-        rs((1, 1), 0, "s")
+        rs((0, 1), 0, "s")
         s2((0, 1), 0)
+        rs((1, 1), 0, "g")
         fv((0, 1), 0)
+        rs((0, 1), 1, "s")
         s2((0, 1), 1)
         st((0, 1), 0)
         fe((0, 1), 1)

@@ -18,6 +18,7 @@ COPY = mybir.ActivationFunctionType.Copy
 P = 128
 HALF = 512
 LATE = ((0, 1), (1, 0), (1, 1),)
+WHOLE = (("X", 1), ("h", 1),)
 
 
 def tile_graphconvolution_kernel(tc, prott5_emd, adj, h0, weight, lamda, alpha, l, out):
@@ -53,11 +54,18 @@ def tile_graphconvolution_kernel(tc, prott5_emd, adj, h0, weight, lamda, alpha, 
             tagn = "%d%d" % u
             r_sb[u] = keep.tile([P, 4, HALF], F32, name="r" + tagn)
         s_all, w_all, x_all = {}, {}, {}
-        x_in, h0_in, w_in = {}, {}, {}
+        raw = {}
+        for kind in "XhW":
+            for k in range(2):
+                if (kind, k) in WHOLE:
+                    whole = keep.tile([P, 4, 2 * HALF], BF16, name="raw%s%d" % (kind, k))
+                    raw[(kind, k)] = whole
+                    raw[(kind, k, 0)], raw[(kind, k, 1)] = whole[:, :, 0:HALF], whole[:, :, HALF : 2 * HALF]
+                else:
+                    for c in range(2):
+                        half = keep.tile([P, 4, HALF], BF16, name="raw%s%d%d" % (kind, k, c))
+                        raw[(kind, k, c)] = half[:]
         for k in range(2):
-            x_in[k] = keep.tile([P, 4, 2 * HALF], BF16, name="xin%d" % k)
-            h0_in[k] = keep.tile([P, 4, 2 * HALF], BF16, name="h0in%d" % k)
-            w_in[k] = keep.tile([P, 4, 2 * HALF], BF16, name="win%d" % k)
             sg = keep.tile([P, 2, 4, P, 4], BF16, name="sg%d" % k, align_bytes=64)
             sc = keep.tile([P, 2 * HALF], U32, name="sc%d" % k, align_bytes=64)
             ss = keep.tile([P, 2 * HALF], U8, name="ss%d" % k, align_bytes=64)
@@ -72,7 +80,7 @@ def tile_graphconvolution_kernel(tc, prott5_emd, adj, h0, weight, lamda, alpha, 
             w_all[k] = (wc, ws, wg)
             for c in range(2):
                 part = slice(HALF * c, HALF * c + HALF)
-                xraw[(k, c)], h0_sb[(k, c)], wraw[(k, c)] = x_in[k][:, :, part], h0_in[k][:, :, part], w_in[k][:, :, part]
+                xraw[(k, c)], h0_sb[(k, c)], wraw[(k, c)] = raw[("X", k, c)], raw[("h", k, c)], raw[("W", k, c)]
                 sgr[(k, c)], s_codes[(k, c)], s_plane[(k, c)] = sg[:, c], sc[:, part], ss[:, part]
                 xgr[(k, c)], x_codes[(k, c)], x_plane[(k, c)] = xg[:, c], xc[:, part], xs[:, part]
                 wgr[(c, k)], w_codes[(c, k)], w_plane[(c, k)] = wg[:, c], wc[:, part], ws[:, part]
@@ -86,19 +94,18 @@ def tile_graphconvolution_kernel(tc, prott5_emd, adj, h0, weight, lamda, alpha, 
             if name == "adj":
                 nc.sync.dma_start(out=adj_sb[:], in_=adj.rearrange("(p i) m -> p (i m)", i=4))
                 return
-            a = int(name[1])
-            cols = slice(0, 2 * HALF) if len(name) == 2 else slice(HALF * int(name[2]), HALF * int(name[2]) + HALF)
-            if name[0] == "X":
-                nc.sync.dma_start(
-                    out=x_in[a][:, :, cols], in_=prott5_emd[a].rearrange("(p j) f -> p j f", j=4)[:, :, cols]
-                )
-            elif name[0] == "h":
-                nc.sync.dma_start(out=h0_in[a][:, :, cols], in_=h0[a].rearrange("(p i) f -> p i f", i=4)[:, :, cols])
+            kind, a = name[0], int(name[1])
+            if len(name) == 2:
+                dst, cols = raw[(kind, a)][:], slice(0, 2 * HALF)
             else:
-                nc.sync.dma_start(
-                    out=w_in[a][:, :, cols],
-                    in_=weight[HALF * a : HALF * a + HALF, cols].rearrange("(j p) o -> p j o", p=P),
-                )
+                c = int(name[2])
+                dst, cols = raw[(kind, a, c)], slice(HALF * c, HALF * c + HALF)
+            if kind == "W":
+                src = weight[HALF * a : HALF * a + HALF, cols].rearrange("(j p) o -> p j o", p=P)
+            else:
+                rows = prott5_emd[a] if kind == "X" else h0[a]
+                src = rows.rearrange("(p j) f -> p j f", j=4)[:, :, cols]
+            nc.sync.dma_start(out=dst, in_=src)
 
         def ta(hn):
             t2 = tpp.tile([P, 2, 256], F32, name="pa%d" % hn, tag="tp")
@@ -317,6 +324,7 @@ def tile_graphconvolution_kernel(tc, prott5_emd, adj, h0, weight, lamda, alpha, 
         s1((0, 0), 1)
         ld("W10")
         p1((0, 0), 0)
+        rx((1, 1), "s")
         s1((0, 0), 2)
         ld("h1")
         p1((0, 0), 1)
@@ -330,7 +338,6 @@ def tile_graphconvolution_kernel(tc, prott5_emd, adj, h0, weight, lamda, alpha, 
         s1((0, 1), 0)
         ld("W01")
         p1((0, 1), 0)
-        rx((1, 1), "s")
         t((0, 0), 1)
         evt((0, 0), 1)
         s1((0, 1), 1)
@@ -393,7 +400,7 @@ def tile_graphconvolution_kernel(tc, prott5_emd, adj, h0, weight, lamda, alpha, 
         evt((1, 1), 2)
         t((1, 1), 3)
         evt((1, 1), 3)
-        wx(3)
+        wx(2)
         qS(1)
         rw((1, 1), "s")
         s2((0, 0), 0)
@@ -445,16 +452,15 @@ def tile_graphconvolution_kernel(tc, prott5_emd, adj, h0, weight, lamda, alpha, 
         fv((0, 1), 3)
         s2((1, 1), 0)
         st((0, 1), 3)
-        fe((1, 1), 0)
+        fv((1, 1), 0)
         s2((1, 1), 1)
-        fg((1, 1), 0)
-        st((0, 1), 1)
+        st((1, 1), 0)
         fv((1, 1), 1)
         s2((1, 1), 2)
         st((1, 1), 1)
         fv((1, 1), 2)
         s2((1, 1), 3)
-        st((1, 1), 2)
+        st((0, 1), 1)
         fv((1, 1), 3)
-        st((1, 1), 0)
+        st((1, 1), 2)
         st((1, 1), 3)

import math
from contextlib import ExitStack

import concourse.mybir as mybir
from concourse.masks import make_identity

FLOPS = 2 * 2 * 512 * 512 * 1024 + 2 * 2 * 512 * 1024 * 1024

F32 = mybir.dt.float32
BF16 = mybir.dt.bfloat16
U32 = mybir.dt.uint32
U8 = mybir.dt.uint8
FP8X4 = mybir.dt.float8_e4m3fn_x4
MULT = mybir.AluOpType.mult
ADD = mybir.AluOpType.add
COPY = mybir.ActivationFunctionType.Copy

P = 128
HALF = 512
LATE = ((0, 1), (1, 0), (1, 1),)
WHOLE = (("X", 1), ("h", 1),)


def tile_graphconvolution_kernel(tc, prott5_emd, adj, h0, weight, lamda, alpha, l, out):
    nc = tc.nc
    theta = min(1.0, math.log(lamda / l + 1.0))
    assert 0.0 < alpha and theta < 1.0
    hi_gain = (1.0 - alpha) * (1.0 - theta)
    h0_gain = alpha * (1.0 - theta)
    back_gain = 1.0 / (1.0 - theta)
    units = [(0, 0), (0, 1), (1, 0), (1, 1)]

    with ExitStack() as ctx:
        keep = ctx.enter_context(tc.tile_pool(name="keep", bufs=1))
        stage = ctx.enter_context(tc.tile_pool(name="stage", bufs=3))
        accp = ctx.enter_context(tc.psum_pool(name="accp", bufs=4))
        tpp = ctx.enter_context(tc.psum_pool(name="tpp", bufs=4))
        ctx.enter_context(tc.manual_schedule())

        ident = keep.tile([P, P], F32, name="ident")
        make_identity(nc, ident[:])
        warm_sb = keep.tile([P, HALF], BF16, name="warm_sb")
        nc.vector.memset(warm_sb[:], 0.0)

        adj_sb = keep.tile([P, 4 * 512], BF16, name="adj_sb")
        agr = keep.tile([P, 2048], BF16, name="agr", align_bytes=64)
        a_codes = keep.tile([P, 512], U32, name="a_codes", align_bytes=64)
        a_plane = keep.tile([P, 512], U8, name="a_plane", align_bytes=64)
        xraw, xgr, x_codes, x_plane = {}, {}, {}, {}
        h0_sb, r_sb = {}, {}
        sgr, s_codes, s_plane = {}, {}, {}
        wraw, wgr, w_codes, w_plane = {}, {}, {}, {}
        for u in units:
            tagn = "%d%d" % u
            r_sb[u] = keep.tile([P, 4, HALF], F32, name="r" + tagn)
        s_all, w_all, x_all = {}, {}, {}
        raw = {}
        for kind in "XhW":
            for k in range(2):
                if (kind, k) in WHOLE:
                    whole = keep.tile([P, 4, 2 * HALF], BF16, name="raw%s%d" % (kind, k))
                    raw[(kind, k)] = whole
                    raw[(kind, k, 0)], raw[(kind, k, 1)] = whole[:, :, 0:HALF], whole[:, :, HALF : 2 * HALF]
                else:
                    for c in range(2):
                        half = keep.tile([P, 4, HALF], BF16, name="raw%s%d%d" % (kind, k, c))
                        raw[(kind, k, c)] = half[:]
        for k in range(2):
            sg = keep.tile([P, 2, 4, P, 4], BF16, name="sg%d" % k, align_bytes=64)
            sc = keep.tile([P, 2 * HALF], U32, name="sc%d" % k, align_bytes=64)
            ss = keep.tile([P, 2 * HALF], U8, name="ss%d" % k, align_bytes=64)
            wg = keep.tile([P, 2, HALF, 4], BF16, name="wg%d" % k, align_bytes=64)
            wc = keep.tile([P, 2 * HALF], U32, name="wc%d" % k, align_bytes=64)
            ws = keep.tile([P, 2 * HALF], U8, name="ws%d" % k, align_bytes=64)
            xg = keep.tile([P, 2, HALF, 4], BF16, name="xg%d" % k, align_bytes=64)
            xc = keep.tile([P, 2 * HALF], U32, name="xc%d" % k, align_bytes=64)
            xs = keep.tile([P, 2 * HALF], U8, name="xs%d" % k, align_bytes=64)
            x_all[k] = (xc, xs, xg)
            s_all[k] = (sc, ss, sg)
            w_all[k] = (wc, ws, wg)
            for c in range(2):
                part = slice(HALF * c, HALF * c + HALF)
                xraw[(k, c)], h0_sb[(k, c)], wraw[(k, c)] = raw[("X", k, c)], raw[("h", k, c)], raw[("W", k, c)]
                sgr[(k, c)], s_codes[(k, c)], s_plane[(k, c)] = sg[:, c], sc[:, part], ss[:, part]
                xgr[(k, c)], x_codes[(k, c)], x_plane[(k, c)] = xg[:, c], xc[:, part], xs[:, part]
                wgr[(c, k)], w_codes[(c, k)], w_plane[(c, k)] = wg[:, c], wc[:, part], ws[:, part]

        adj_words = adj_sb[:].bitcast(F32).rearrange("p (i w u) -> p i w u", i=4, u=2)
        agr_words = agr[:].bitcast(F32).rearrange("p (n u) -> p n u", u=2)
        live = {}
        banks = []

        def ld(name):
            if name == "adj":
                nc.sync.dma_start(out=adj_sb[:], in_=adj.rearrange("(p i) m -> p (i m)", i=4))
                return
            kind, a = name[0], int(name[1])
            if len(name) == 2:
                dst, cols = raw[(kind, a)][:], slice(0, 2 * HALF)
            else:
                c = int(name[2])
                dst, cols = raw[(kind, a, c)], slice(HALF * c, HALF * c + HALF)
            if kind == "W":
                src = weight[HALF * a : HALF * a + HALF, cols].rearrange("(j p) o -> p j o", p=P)
            else:
                rows = prott5_emd[a] if kind == "X" else h0[a]
                src = rows.rearrange("(p j) f -> p j f", j=4)[:, :, cols]
            nc.sync.dma_start(out=dst, in_=src)

        def ta(hn):
            t2 = tpp.tile([P, 2, 256], F32, name="pa%d" % hn, tag="tp")
            live[("pa", hn)] = t2
            for k in range(2):
                for w in range(2):
                    nc.tensor.transpose(t2[:, w, P * k : P * k + P], adj_words[:, 2 * hn + k, :, w], ident[:])

        def eva(hn, eng):
            dst = agr_words[:, 256 * hn : 256 * hn + 256, :]
            src = live[("pa", hn)][:].rearrange("p u n -> p n u")
            if eng == "s":
                nc.scalar.copy(out=dst, in_=src)
            else:
                nc.vector.tensor_copy(out=dst, in_=src)

        def regroup(eng, dst, src):
            if eng == "v":
                nc.vector.tensor_copy(
                    out=dst[:].rearrange("p (c i) t -> p c t i", i=4),
                    in_=src[:].rearrange("p t (c i) -> p c t i", i=4),
                )
            elif eng == "s":
                nc.scalar.copy(
                    out=dst[:].rearrange("p (c i) t -> p c t i", i=4),
                    in_=src[:].rearrange("p t (c i) -> p c t i", i=4),
                )
            else:
                nc.gpsimd.tensor_scalar(
                    out=dst[:], in0=src[:].rearrange("p t w -> p w t"), scalar1=1.0, scalar2=0.0, op0=MULT, op1=ADD
                )

        def quant(codes, plane, grouped2d):
            nc.vector.quantize_mx(out=codes[:].bitcast(FP8X4), scales=plane[:], in_=grouped2d)

        def qa():
            quant(a_codes, a_plane, agr[:])

        def rx(u, eng):
            regroup(eng, xgr[u], xraw[u])

        def rw(u, eng):
            regroup(eng, wgr[u], wraw[u])

        def qx(u):
            quant(x_codes[u], x_plane[u], xgr[u].rearrange("p w j -> p (w j)"))

        def qw(u):
            quant(w_codes[u], w_plane[u], wgr[u].rearrange("p w j -> p (w j)"))

        def qS(b):
            codes, plane, grouped = s_all[b]
            quant(codes, plane, grouped[:].rearrange("p c i n j -> p (c i n j)"))

        def qX(b):
            codes, plane, grouped = x_all[b]
            quant(codes, plane, grouped[:].rearrange("p h w j -> p (h w j)"))

        def qW(h):
            codes, plane, grouped = w_all[h]
            quant(codes, plane, grouped[:].rearrange("p c w j -> p (c w j)"))

        def qs(u):
            quant(s_codes[u], s_plane[u], sgr[u].rearrange("p i n j -> p (i n j)"))

        def ps(u, hp, eng):
            dst = r_sb[u][:, 2 * hp : 2 * hp + 2, :]
            src = h0_sb[u][:, 2 * hp : 2 * hp + 2, :]
            if eng == "g":
                nc.gpsimd.tensor_scalar(out=dst, in0=src, scalar1=h0_gain, scalar2=0.0, op0=MULT, op1=ADD)
            elif eng == "v":
                nc.vector.tensor_scalar(out=dst, in0=src, scalar1=h0_gain, scalar2=0.0, op0=MULT, op1=ADD)
            else:
                nc.scalar.activation(out=dst, in_=src, func=COPY, scale=h0_gain)

        def next_bank():
            bank = live.pop("next", None)
            if bank is None:
                bank = accp.tile([P, HALF], F32, name="bank%d" % len(banks), tag="acc")
                banks.append(bank)
            return bank

        def wa(count):
            bank = next_bank()
            live["next"] = bank
            for k in range(count):
                nc.tensor.matmul(bank[:], warm_sb[:, 0:P], warm_sb[:], start=True, stop=True)

        def wx(count):
            bank = next_bank()
            live["next"] = bank
            codes, plane = x_codes[(0, 0)], x_plane[(0, 0)]
            for k in range(count):
                nc.tensor.matmul_mx(
                    out=bank[:],
                    lhsT=codes[:, 0:P].bitcast(FP8X4),
                    lhsT_scale=plane[:, 0:P],
                    rhs=codes[:].bitcast(FP8X4),
                    rhs_scale=plane[:],
                    start=True,
                    stop=True,
                )

        def s1(u, i):
            a = next_bank()
            live[(1, u, i)] = a
            nc.tensor.matmul_mx(
                out=a[:],
                lhsT=a_codes[:, P * i : P * i + P].bitcast(FP8X4),
                lhsT_scale=a_plane[:, P * i : P * i + P],
                rhs=x_codes[u][:].bitcast(FP8X4),
                rhs_scale=x_plane[u][:],
                start=True,
                stop=True,
            )

        def p1(u, i):
            acc = live[(1, u, i)][:]
            r = r_sb[u][:, i, :]
            if u in LATE:
                nc.vector.scalar_tensor_tensor(
                    out=r, in0=h0_sb[u][:, i, :], scalar=alpha / (1.0 - alpha), in1=acc, op0=MULT, op1=ADD
                )
            else:
                nc.vector.scalar_tensor_tensor(out=r, in0=acc, scalar=hi_gain, in1=r, op0=MULT, op1=ADD)

        def rs(u, hp, eng):
            r = r_sb[u][:, 2 * hp : 2 * hp + 2, :]
            if eng == "g":
                nc.gpsimd.tensor_scalar(out=r, in0=r, scalar1=hi_gain, scalar2=0.0, op0=MULT, op1=ADD)
            elif eng == "v":
                nc.vector.tensor_scalar(out=r, in0=r, scalar1=hi_gain, scalar2=0.0, op0=MULT, op1=ADD)
            else:
                nc.scalar.activation(out=r, in_=r, func=COPY, scale=hi_gain)

        def t(u, i):
            tp = tpp.tile([P, 4, P], F32, name="tp_%d%d%d" % (u[0], u[1], i), tag="tp")
            live[("tp", u, i)] = tp
            for j in range(4):
                nc.tensor.transpose(tp[:, j, :], r_sb[u][:, i, P * j : P * j + P], ident[:])

        def evt(u, i):
            nc.scalar.activation(
                out=sgr[u][:, i, :, :],
                in_=live[("tp", u, i)][:].rearrange("p j n -> p n j"),
                func=COPY,
                scale=(1.0 - alpha) if u in LATE else back_gain,
            )

        def s2(u, i):
            b, h = u
            a = next_bank()
            live[(2, u, i)] = a
            for c in range(2):
                nc.tensor.matmul_mx(
                    out=a[:],
                    lhsT=s_codes[(b, c)][:, P * i : P * i + P].bitcast(FP8X4),
                    lhsT_scale=s_plane[(b, c)][:, P * i : P * i + P],
                    rhs=w_codes[(c, h)][:].bitcast(FP8X4),
                    rhs_scale=w_plane[(c, h)][:],
                    start=(c == 0),
                    stop=(c == 1),
                )

        def fv(u, i):
            nc.vector.scalar_tensor_tensor(
                out=r_sb[u][:, i, :], in0=live[(2, u, i)][:], scalar=theta, in1=r_sb[u][:, i, :], op0=MULT, op1=ADD
            )

        def fe(u, i):
            ut = stage.tile([P, HALF], F32, name="u_%d%d%d" % (u[0], u[1], i), tag="u")
            live[("u", u, i)] = ut
            nc.scalar.activation(out=ut[:], in_=live[(2, u, i)][:], func=COPY, scale=theta)

        def fg(u, i):
            nc.gpsimd.tensor_tensor(out=r_sb[u][:, i, :], in0=live[("u", u, i)][:], in1=r_sb[u][:, i, :], op=ADD)

        def hold(what, u, i=0):
            if what == "qS":
                nc.gpsimd.memset(s_all[u][2][:, 0, 0, 0, 0:2], 0.0)
            elif what == "qW":
                nc.gpsimd.memset(w_all[u][2][:, 0, 0, 0:2], 0.0)
            elif what == "qx":
                nc.gpsimd.memset(xgr[u][:, 0, 0:2], 0.0)
            elif what == "rw":
                nc.gpsimd.memset(wraw[u][:, 0, 0:2], 0.0)

        def st(u, i):
            b, h = u
            nc.sync.dma_start(
                out=out[b].rearrange("(p i) o -> p i o", i=4)[:, i, HALF * h : HALF * h + HALF],
                in_=r_sb[u][:, i, :],
            )

        ld("X00")
        rx((0, 0), "v")
        wa(7)
        ld("adj")
        qx((0, 0))
        ta(0)
        ld("X01")
        rx((0, 1), "v")
        eva(0, "s")
        ta(1)
        ld("h00")
        eva(1, "s")
        wx(4)
        ld("X1")
        qa()
        ps((0, 0), 0, "s")
        s1((0, 0), 0)
        rx((1, 0), "g")
        ld("h01")
        qx((0, 1))
        ps((0, 0), 1, "s")
        s1((0, 0), 1)
        ld("W10")
        p1((0, 0), 0)
        rx((1, 1), "s")
        s1((0, 0), 2)
        ld("h1")
        p1((0, 0), 1)
        s1((0, 0), 3)
        ld("W00")
        p1((0, 0), 2)
        t((0, 0), 0)
        ld("W11")
        p1((0, 0), 3)
        evt((0, 0), 0)
        s1((0, 1), 0)
        ld("W01")
        p1((0, 1), 0)
        t((0, 0), 1)
        evt((0, 0), 1)
        s1((0, 1), 1)
        p1((0, 1), 1)
        s1((0, 1), 2)
        qx((1, 0))
        t((0, 0), 2)
        qx((1, 1))
        evt((0, 0), 2)
        t((0, 0), 3)
        hold("qx", (1, 1))
        p1((0, 1), 2)
        evt((0, 0), 3)
        s1((0, 1), 3)
        rw((1, 0), "g")
        p1((0, 1), 3)
        wx(3)
        rw((0, 0), "g")
        t((0, 1), 0)
        evt((0, 1), 0)
        t((0, 1), 1)
        evt((0, 1), 1)
        s1((1, 0), 0)
        p1((1, 0), 0)
        s1((1, 0), 1)
        p1((1, 0), 1)
        s1((1, 0), 2)
        p1((1, 0), 2)
        t((0, 1), 2)
        evt((0, 1), 2)
        t((0, 1), 3)
        evt((0, 1), 3)
        s1((1, 0), 3)
        p1((1, 0), 3)
        s1((1, 1), 0)
        p1((1, 1), 0)
        t((1, 0), 0)
        evt((1, 0), 0)
        t((1, 0), 1)
        evt((1, 0), 1)
        s1((1, 1), 1)
        p1((1, 1), 1)
        s1((1, 1), 2)
        p1((1, 1), 2)
        t((1, 0), 2)
        evt((1, 0), 2)
        t((1, 0), 3)
        evt((1, 0), 3)
        s1((1, 1), 3)
        p1((1, 1), 3)
        wx(1)
        qS(0)
        t((1, 1), 0)
        qW(0)
        evt((1, 1), 0)
        t((1, 1), 1)
        evt((1, 1), 1)
        wx(1)
        t((1, 1), 2)
        evt((1, 1), 2)
        t((1, 1), 3)
        evt((1, 1), 3)
        wx(2)
        qS(1)
        rw((1, 1), "s")
        s2((0, 0), 0)
        hold("qS", 1)
        fv((0, 0), 0)
        rs((1, 0), 0, "s")
        s2((0, 0), 1)
        rw((0, 1), "g")
        st((0, 0), 0)
        fv((0, 0), 1)
        rs((1, 0), 1, "s")
        s2((0, 0), 2)
        st((0, 0), 1)
        fv((0, 0), 2)
        s2((0, 0), 3)
        st((0, 0), 2)
        fv((0, 0), 3)
        s2((1, 0), 0)
        st((0, 0), 3)
        fv((1, 0), 0)
        s2((1, 0), 1)
        st((1, 0), 0)
        qW(1)
        s2((1, 0), 2)
        hold("qW", 1)
        fv((1, 0), 1)
        s2((1, 0), 3)
        st((1, 0), 1)
        fv((1, 0), 2)
        fe((1, 0), 3)
        wx(4)
        fg((1, 0), 3)
        st((1, 0), 2)
        rs((0, 1), 0, "s")
        s2((0, 1), 0)
        rs((1, 1), 0, "g")
        fv((0, 1), 0)
        rs((0, 1), 1, "s")
        s2((0, 1), 1)
        st((0, 1), 0)
        fe((0, 1), 1)
        s2((0, 1), 2)
        fg((0, 1), 1)
        st((1, 0), 3)
        fv((0, 1), 2)
        rs((1, 1), 1, "s")
        s2((0, 1), 3)
        st((0, 1), 2)
        fv((0, 1), 3)
        s2((1, 1), 0)
        st((0, 1), 3)
        fv((1, 1), 0)
        s2((1, 1), 1)
        st((1, 1), 0)
        fv((1, 1), 1)
        s2((1, 1), 2)
        st((1, 1), 1)
        fv((1, 1), 2)
        s2((1, 1), 3)
        st((0, 1), 1)
        fv((1, 1), 3)
        st((1, 1), 2)
        st((1, 1), 3)
